import numpy as np
import ml_dtypes


def mxq(x, axis, fmt="e4m3"):
    dtype, down = {"e4m3": (ml_dtypes.float8_e4m3fn, 7), "e5m2": (ml_dtypes.float8_e5m2, 14)}[fmt]
    v = np.moveaxis(np.asarray(x, np.float32).astype(ml_dtypes.bfloat16).astype(np.float64), axis, -1)
    blocks = v.reshape(v.shape[:-1] + (-1, 32))
    amax = np.abs(blocks).max(-1, keepdims=True)
    byte = np.maximum(np.where(amax > 0, np.frexp(amax)[1] - 1 + 127, 0) - down, 1)
    scale = np.exp2(byte - 127.0)
    codes = (blocks / scale).astype(np.float32).astype(dtype).astype(np.float64)
    return np.moveaxis((codes * scale).reshape(v.shape), -1, axis)


WIDE = False


def mx_kscale(k):
    if not WIDE:
        return np.ones(k)
    levels = np.array([10, -10, 5, -5, 0])
    a = np.random.permutation(np.resize(levels, k // 512 * 4)).reshape(k // 512, 4)
    idx = np.arange(k)
    return np.exp2(a[idx // 512, idx % 128 // 32])


BF16 = ml_dtypes.bfloat16


def bf(x):
    return np.asarray(x, np.float32).astype(BF16)


def f64(x):
    return np.asarray(x).astype(np.float64)


E2M1 = np.array([0.0, 0.5, 1.0, 1.5, 2.0, 3.0, 4.0, 6.0, -0.0, -0.5, -1.0, -1.5, -2.0, -3.0, -4.0, -6.0])


def pack_weight(w, fmt):
    k, n = w.shape
    w = f64(bf(w)).reshape(k // 32, 32, n)
    amax = np.abs(w).max(1)
    if fmt == "e4m3":
        byte = np.frexp(amax)[1] - 1 + 127 - 7
    else:
        mant, ex = np.frexp(amax / 6.0)
        byte = np.where(mant > 0.5, ex, ex - 1) + 127
    byte = np.clip(np.where(amax > 0, byte, 1), 1, 254)
    scaled = (w * np.exp2(127.0 - byte)[:, None, :]).reshape(k, n).astype(np.float32)
    by_word = np.ascontiguousarray(scaled.reshape(k // 512, 128, 4, n).transpose(0, 1, 3, 2))
    if fmt == "e4m3":
        words = by_word.astype(ml_dtypes.float8_e4m3fn).view(np.uint8)
    else:
        c = by_word.astype(ml_dtypes.float4_e2m1fn).view(np.uint8) & 0xF
        words = c[..., 0::2] | (c[..., 1::2] << 4)
    return np.ascontiguousarray(words), np.ascontiguousarray(byte.astype(np.uint8).reshape(k // 512, 16, n))


def unpack_weight(words, scales, fmt):
    g, p, n, _ = words.shape
    if fmt == "e4m3":
        vals = np.ascontiguousarray(words).view(ml_dtypes.float8_e4m3fn).astype(np.float64)
    else:
        nib = np.empty((g, p, n, 4), np.uint8)
        nib[..., 0::2] = words & 0xF
        nib[..., 1::2] = words >> 4
        vals = E2M1[nib]
    vals = vals * np.repeat(np.exp2(scales.astype(np.float64) - 127.0), 8, axis=1)[..., None]
    return vals.transpose(0, 1, 3, 2).reshape(g * 512, n)


B, In, H, Hh, E, G = 512, 1024, 1024, 256, 128, 4
EPS = 1e-6


def rn(*shape):
    return np.random.standard_normal(shape)


def sigmoid(v):
    return 1.0 / (1.0 + np.exp(-v))


def ln(a, gamma, beta):
    mean = a.mean(-1, keepdims=True)
    std = a.std(-1, keepdims=True, ddof=1)
    return gamma * (a - mean) / (std + EPS) + beta


def expand(emb, w):
    return (emb.transpose(1, 0, 2) @ w.transpose(0, 2, 1)).transpose(1, 0, 2)


def setup_inputs():
    s, t = mx_kscale(In), mx_kscale(H)
    x = bf(rn(B, In) * s)
    h = bf(rn(B, H) * t)
    c = bf(rn(B, H))
    emb_h = bf(1.0 + 0.5 * rn(B, G, E))
    emb_x = bf(1.0 + 0.5 * rn(B, G, E))
    emb_b = bf(rn(B, G, E))
    Wsh = bf(1.0 / E + 0.5 * rn(G, H, E) / np.sqrt(E))
    Wsx = bf(1.0 / E + 0.5 * rn(G, H, E) / np.sqrt(E))
    Wsb = bf(0.5 * rn(G, H, E) / np.sqrt(E))
    Wih_words, Wih_scales = pack_weight((rn(G * H, In) / np.sqrt(In) / s[None, :]).T, 'e4m3')
    Whh_words, Whh_scales = pack_weight((rn(G * H, H) / np.sqrt(H) / t[None, :]).T, 'e4m3')
    bias = bf(0.3 * rn(G * H))
    ln_gamma = bf(1.0 + 0.1 * rn(G, H))
    ln_beta = bf(0.1 * rn(G, H))
    lnc_gamma = bf(1.0 + 0.1 * rn(H))
    lnc_beta = bf(0.1 * rn(H))
    return {
        'x': x,
        'h': h,
        'c': c,
        'emb_h': emb_h,
        'emb_x': emb_x,
        'emb_b': emb_b,
        'Wsh': Wsh,
        'Wsx': Wsx,
        'Wsb': Wsb,
        'Wih_words': Wih_words,
        'Wih_scales': Wih_scales,
        'Whh_words': Whh_words,
        'Whh_scales': Whh_scales,
        'bias': bias,
        'ln_gamma': ln_gamma,
        'ln_beta': ln_beta,
        'lnc_gamma': lnc_gamma,
        'lnc_beta': lnc_beta,
    }


def reference(x, h, c, emb_h, emb_x, emb_b, Wsh, Wsx, Wsb, Wih_words, Wih_scales, Whh_words, Whh_scales, bias, ln_gamma, ln_beta, lnc_gamma, lnc_beta):
    zh = expand(f64(emb_h), f64(Wsh))
    zx = expand(f64(emb_x), f64(Wsx))
    zb = expand(f64(emb_b), f64(Wsb))
    xh = (mxq(f64(x), 1, 'e4m3') @ unpack_weight(Wih_words, Wih_scales, 'e4m3')).reshape(B, G, H)
    hh = (mxq(f64(h), 1, 'e4m3') @ unpack_weight(Whh_words, Whh_scales, 'e4m3')).reshape(B, G, H)
    gates = xh * zx + hh * zh + (f64(bias).reshape(G, H) + zb)
    gates = ln(gates, f64(ln_gamma), f64(ln_beta))
    i, f, g, o = gates[:, 0], gates[:, 1], gates[:, 2], gates[:, 3]
    new_c = f64(c) * sigmoid(f) + sigmoid(i) * np.tanh(g)
    new_c = ln(new_c, f64(lnc_gamma), f64(lnc_beta))
    new_h = np.tanh(new_c) * sigmoid(o)
    return new_h, new_c

@@ -1,0 +1,287 @@
+from contextlib import ExitStack
+
+import concourse.mybir as mybir
+from concourse.masks import make_identity
+
+F32 = mybir.dt.float32
+BF16 = mybir.dt.bfloat16
+U32 = mybir.dt.uint32
+U8 = mybir.dt.uint8
+I32 = mybir.dt.int32
+FP8X4 = mybir.dt.float8_e4m3fn_x4
+ALU = mybir.AluOpType
+ACT = mybir.ActivationFunctionType
+
+P = 128
+B = 512
+K = 1024
+H = 1024
+G = 4
+E = 128
+EPS = 1e-6
+
+B_TILES = B // P
+K_PASS = 4 * P
+PASSES = K // K_PASS
+N_TILE = 512
+HALVES = H // N_TILE
+UNIT_BLOCKS = H // P
+
+GATE_I, GATE_F, GATE_G, GATE_O = 0, 1, 2, 3
+GATE_ORDER = (GATE_I, GATE_G, GATE_F, GATE_O)
+
+FLOPS = 2 * 2 * B * K * G * H + 3 * 2 * B * G * H * E
+
+
+def tile_hyperlstmcell_pb_kernel(
+    tc,
+    x,
+    h,
+    c,
+    emb_h,
+    emb_x,
+    emb_b,
+    Wsh,
+    Wsx,
+    Wsb,
+    Wih_words,
+    Wih_scales,
+    Whh_words,
+    Whh_scales,
+    bias,
+    ln_gamma,
+    ln_beta,
+    lnc_gamma,
+    lnc_beta,
+    out_0,
+    out_1,
+):
+    nc = tc.nc
+    with ExitStack() as ctx:
+        const = ctx.enter_context(tc.tile_pool(name="const", bufs=1))
+        per_gate = ctx.enter_context(tc.tile_pool(name="per_gate", bufs=2))
+        work = ctx.enter_context(tc.tile_pool(name="work", bufs=3))
+        gates = ctx.enter_context(tc.tile_pool(name="gates", bufs=3))
+        small = ctx.enter_context(tc.tile_pool(name="small", bufs=4))
+        stage = ctx.enter_context(tc.tile_pool(name="stage", bufs=4))
+        late = ctx.enter_context(tc.tile_pool(name="late", bufs=B_TILES))
+        psum_one = ctx.enter_context(tc.psum_pool(name="psum_one", bufs=1))
+        psum_two = ctx.enter_context(tc.psum_pool(name="psum_two", bufs=2))
+
+        ident_bf = const.tile([P, P], BF16)
+        make_identity(nc, ident_bf[:])
+        ident_f32 = const.tile([P, P], F32)
+        make_identity(nc, ident_f32[:])
+        one_half = const.tile([P, 1], F32)
+        nc.vector.memset(one_half[:], 0.5)
+        warm = const.tile([P, 1], F32)
+        nc.scalar.activation(out=warm[:], in_=one_half[:], func=ACT.Sigmoid)
+
+        planes = const.tile([P, G * H], U8, align_bytes=64)
+        nc.vector.memset(planes[:].bitcast(I32), 0)
+
+        act_codes = const.tile([P, 2, B_TILES, PASSES, P], U32, align_bytes=64)
+        act_scales = const.tile([P, 2, B_TILES, PASSES, P], U8, align_bytes=64)
+        emb_t = [const.tile([P, G, B], BF16, name="emb_t%d" % i) for i in range(3)]
+        c_sb = const.tile([P, B_TILES, H], BF16)
+
+        for bt in range(B_TILES):
+            rows = slice(bt * P, (bt + 1) * P)
+            for operand, source in enumerate((x, h)):
+                raw = stage.tile([P, K], BF16)
+                nc.sync.dma_start(out=raw[:], in_=source[rows, :])
+                words = raw[:].bitcast(F32)
+                flipped = psum_two.tile([P, PASSES, 2, P], F32, tag="flip")
+                for g in range(PASSES):
+                    for u in range(2):
+                        nc.tensor.transpose(
+                            flipped[:, g, u, :],
+                            words[:, 256 * g + u : 256 * (g + 1) : 2],
+                            ident_f32[:],
+                        )
+                grouped = stage.tile([P, PASSES * P * 4], BF16, align_bytes=64)
+                nc.vector.tensor_copy(
+                    out=grouped[:].bitcast(F32).rearrange("p (g b u) -> p g b u", g=PASSES, u=2),
+                    in_=flipped[:].rearrange("p g u b -> p g b u"),
+                )
+                nc.vector.quantize_mx(
+                    out=act_codes[:, operand, bt].rearrange("p g b -> p (g b)").bitcast(FP8X4),
+                    scales=act_scales[:, operand, bt].rearrange("p g b -> p (g b)"),
+                    in_=grouped[:],
+                )
+            for i, source in enumerate((emb_x, emb_h, emb_b)):
+                emb_raw = stage.tile([P, G, E], BF16)
+                nc.sync.dma_start(out=emb_raw[:], in_=source[rows])
+                emb_flip = psum_two.tile([P, G, P], BF16, tag="flip")
+                for gate in range(G):
+                    nc.tensor.transpose(emb_flip[:, gate, :], emb_raw[:, gate, :], ident_bf[:])
+                nc.scalar.copy(out=emb_t[i][:, :, rows], in_=emb_flip[:])
+
+        for operand, source in enumerate((Wih_scales, Whh_scales)):
+            for quad in range(4):
+                first = 32 * quad + 8 * operand
+                nc.sync.dma_start(
+                    out=planes[first : first + 8, :].bitcast(I32),
+                    in_=source[:, 4 * quad : 4 * quad + 4, :].bitcast(I32),
+                )
+
+        bias_bc = const.tile([P, G, H], BF16)
+        gamma_bc = const.tile([P, G, H], BF16)
+        beta_bc = const.tile([P, G, H], BF16)
+        nc.scalar.dma_start(out=bias_bc[:].rearrange("p g n -> p (g n)"), in_=bias.partition_broadcast(P))
+        nc.scalar.dma_start(
+            out=gamma_bc[:].rearrange("p g n -> p (g n)"),
+            in_=ln_gamma.rearrange("g n -> (g n)").partition_broadcast(P),
+        )
+        nc.scalar.dma_start(
+            out=beta_bc[:].rearrange("p g n -> p (g n)"),
+            in_=ln_beta.rearrange("g n -> (g n)").partition_broadcast(P),
+        )
+        gamma_c_bc = const.tile([P, H], BF16)
+        beta_c_bc = const.tile([P, H], BF16)
+        nc.scalar.dma_start(out=gamma_c_bc[:], in_=lnc_gamma.partition_broadcast(P))
+        nc.scalar.dma_start(out=beta_c_bc[:], in_=lnc_beta.partition_broadcast(P))
+        nc.sync.dma_start(out=c_sb[:], in_=c.rearrange("(t p) n -> p t n", p=P))
+
+        def norm_scalars(sum_parts, sum_squares):
+            total = small.tile([P, 1], F32)
+            nc.vector.tensor_tensor(out=total[:], in0=sum_parts[:, 0:1], in1=sum_parts[:, 1:2], op=ALU.add)
+            mean = small.tile([P, 1], F32)
+            nc.vector.tensor_scalar(out=mean[:], in0=total[:], scalar1=1.0 / H, scalar2=None, op0=ALU.mult)
+            spread = small.tile([P, 1], F32)
+            nc.vector.scalar_tensor_tensor(
+                out=spread[:], in0=total[:], scalar=mean[:, 0:1], in1=sum_squares[:], op0=ALU.mult, op1=ALU.subtract
+            )
+            variance = small.tile([P, 1], F32)
+            nc.vector.tensor_scalar(
+                out=variance[:], in0=spread[:], scalar1=-1.0 / (H - 1), scalar2=0.0, op0=ALU.mult, op1=ALU.max
+            )
+            std = small.tile([P, 1], F32)
+            nc.gpsimd.tensor_tensor(out=std[:], in0=variance[:], in1=one_half[:], op=ALU.pow)
+            rstd = small.tile([P, 1], F32)
+            nc.vector.tensor_scalar(out=rstd[:], in0=std[:], scalar1=EPS, scalar2=None, op0=ALU.add)
+            nc.vector.reciprocal(out=rstd[:], in_=rstd[:])
+            return mean, rstd
+
+        def sum_of_squares(values):
+            squares = work.tile([P, H], BF16, bufs=2)
+            sum_squares = small.tile([P, 1], F32)
+            nc.scalar.activation(out=squares[:], in_=values, func=ACT.Square, accum_out=sum_squares[:])
+            return sum_squares
+
+        def scale_and_shift(values, mean, rstd, gamma_row, beta_row):
+            nc.vector.scalar_tensor_tensor(
+                out=values, in0=values, scalar=mean[:, 0:1], in1=gamma_row, op0=ALU.subtract, op1=ALU.mult
+            )
+            nc.vector.scalar_tensor_tensor(
+                out=values, in0=values, scalar=rstd[:, 0:1], in1=beta_row, op0=ALU.mult, op1=ALU.add
+            )
+
+        product_ig = [None] * B_TILES
+        tanh_c = [None] * B_TILES
+
+        for gate in GATE_ORDER:
+            w_words = per_gate.tile([P, 2, PASSES, H], U32, align_bytes=64)
+            for operand, source in enumerate((Wih_words, Whh_words)):
+                for g in range(PASSES):
+                    nc.sync.dma_start(
+                        out=w_words[:, operand, g, :].bitcast(I32),
+                        in_=source[g, :, gate * H : (gate + 1) * H, :].rearrange("p n t -> p (n t)").bitcast(I32),
+                    )
+            ws_t = []
+            for i, source in enumerate((Wsx, Wsh, Wsb)):
+                ws_raw = per_gate.tile([P, UNIT_BLOCKS, E], BF16, name="ws_raw%d" % i)
+                nc.sync.dma_start(out=ws_raw[:], in_=source[gate].rearrange("(j p) e -> p j e", p=P))
+                ws_flip = psum_two.tile([P, UNIT_BLOCKS, P], BF16, tag="flip")
+                for j in range(UNIT_BLOCKS):
+                    nc.tensor.transpose(ws_flip[:, j, :], ws_raw[:, j, :], ident_bf[:])
+                flat = per_gate.tile([P, H], BF16, name="ws_t%d" % i)
+                nc.scalar.copy(out=flat[:], in_=ws_flip[:].rearrange("p j n -> p (j n)"))
+                ws_t.append(flat)
+
+            for bt in range(B_TILES):
+                rows = slice(bt * P, (bt + 1) * P)
+                if gate == GATE_I:
+                    pre = late.tile([P, H], F32, tag="product_ig")
+                else:
+                    pre = gates.tile([P, H], F32, tag="pre")
+                sum_parts = small.tile([P, HALVES], F32)
+                for half in range(HALVES):
+                    cols = slice(half * N_TILE, (half + 1) * N_TILE)
+                    all_cols = slice(gate * H + half * N_TILE, gate * H + (half + 1) * N_TILE)
+                    z_ps = []
+                    for i, tag in enumerate(("zx", "zh")):
+                        z = psum_one.tile([P, N_TILE], F32, tag=tag)
+                        nc.tensor.matmul(out=z[:], lhsT=emb_t[i][:, gate, rows], rhs=ws_t[i][:, cols], start=True, stop=True)
+                        z_ps.append(z)
+                    zb_ps = psum_two.tile([P, N_TILE], F32, tag="zb")
+                    nc.tensor.matmul(out=zb_ps[:], lhsT=emb_t[2][:, gate, rows], rhs=ws_t[2][:, cols], start=True, stop=True)
+                    mx_ps = []
+                    for operand, tag in enumerate(("xh", "hh")):
+                        acc = psum_one.tile([P, N_TILE], F32, tag=tag)
+                        for g in range(PASSES):
+                            first = 8 * operand + 4 * g
+                            nc.tensor.matmul_mx(
+                                out=acc[:],
+                                lhsT=act_codes[:, operand, bt, g, :].bitcast(FP8X4),
+                                lhsT_scale=act_scales[:, operand, bt, g, :],
+                                rhs=w_words[:, operand, g, cols].bitcast(FP8X4),
+                                rhs_scale=planes[first:P, all_cols],
+                                start=(g == 0),
+                                stop=(g == PASSES - 1),
+                            )
+                        mx_ps.append(acc)
+
+                    zx_sb = work.tile([P, N_TILE], F32)
+                    nc.scalar.copy(out=zx_sb[:], in_=z_ps[0][:])
+                    term_x = work.tile([P, N_TILE], F32)
+                    nc.vector.tensor_tensor(out=term_x[:], in0=mx_ps[0][:], in1=zx_sb[:], op=ALU.mult)
+                    nc.gpsimd.tensor_tensor(out=term_x[:], in0=term_x[:], in1=bias_bc[:, gate, cols], op=ALU.add)
+                    zh_sb = work.tile([P, N_TILE], F32)
+                    nc.scalar.copy(out=zh_sb[:], in_=z_ps[1][:])
+                    term_h = work.tile([P, N_TILE], F32)
+                    nc.vector.tensor_tensor(out=term_h[:], in0=mx_ps[1][:], in1=zh_sb[:], op=ALU.mult)
+                    nc.gpsimd.tensor_tensor(out=term_x[:], in0=term_x[:], in1=term_h[:], op=ALU.add)
+                    nc.vector.scalar_tensor_tensor(
+                        out=pre[:, cols],
+                        in0=zb_ps[:],
+                        scalar=1.0,
+                        in1=term_x[:],
+                        op0=ALU.mult,
+                        op1=ALU.add,
+                        accum_out=sum_parts[:, half : half + 1],
+                    )
+
+                mean, rstd = norm_scalars(sum_parts, sum_of_squares(pre[:]))
+                scale_and_shift(pre[:], mean, rstd, gamma_bc[:, gate, :], beta_bc[:, gate, :])
+                func = ACT.Tanh if gate == GATE_G else ACT.Sigmoid
+                nc.scalar.activation(out=pre[:], in_=pre[:], func=func)
+
+                if gate == GATE_I:
+                    product_ig[bt] = pre
+                elif gate == GATE_G:
+                    nc.gpsimd.tensor_tensor(out=product_ig[bt][:], in0=product_ig[bt][:], in1=pre[:], op=ALU.mult)
+                elif gate == GATE_F:
+                    cell = product_ig[bt]
+                    nc.vector.tensor_tensor(out=pre[:], in0=pre[:], in1=c_sb[:, bt, :], op=ALU.mult)
+                    cell_sums = small.tile([P, HALVES], F32)
+                    for half in range(HALVES):
+                        cols = slice(half * N_TILE, (half + 1) * N_TILE)
+                        nc.vector.scalar_tensor_tensor(
+                            out=cell[:, cols],
+                            in0=cell[:, cols],
+                            scalar=1.0,
+                            in1=pre[:, cols],
+                            op0=ALU.mult,
+                            op1=ALU.add,
+                            accum_out=cell_sums[:, half : half + 1],
+                        )
+                    mean, rstd = norm_scalars(cell_sums, sum_of_squares(cell[:]))
+                    scale_and_shift(cell[:], mean, rstd, gamma_c_bc[:], beta_c_bc[:])
+                    nc.sync.dma_start(out=out_1[rows, :], in_=cell[:])
+                    squashed = late.tile([P, H], F32, tag="tanh_c")
+                    nc.scalar.activation(out=squashed[:], in_=cell[:], func=ACT.Tanh)
+                    tanh_c[bt] = squashed
+                else:
+                    nc.vector.tensor_tensor(out=tanh_c[bt][:], in0=tanh_c[bt][:], in1=pre[:], op=ALU.mult)
+                    nc.sync.dma_start(out=out_0[rows, :], in_=tanh_c[bt][:])

@@ -11,6 +11,7 @@ I32 = mybir.dt.int32
 FP8X4 = mybir.dt.float8_e4m3fn_x4
 ALU = mybir.AluOpType
 ACT = mybir.ActivationFunctionType
+AXIS = mybir.AxisListType
 
 P = 128
 B = 512
@@ -26,9 +27,22 @@ PASSES = K // K_PASS
 N_TILE = 512
 HALVES = H // N_TILE
 UNIT_BLOCKS = H // P
+BANK_BLOCKS = N_TILE // P
 
 GATE_I, GATE_F, GATE_G, GATE_O = 0, 1, 2, 3
 GATE_ORDER = (GATE_I, GATE_G, GATE_F, GATE_O)
+JOBS = G * B_TILES
+SLOTS = JOBS * HALVES
+
+LAG_SUMS = 3
+LAG_NORMALISE = 4
+LAG_FLIP = 5
+LAG_ACTIVATE = 6
+LAG_CELL = 7
+LAG_UNFLIP = 8
+LAG_CELL_SUMS = 9
+LAG_CELL_NORM = 10
+LAG_CELL_TANH = 11
 
 FLOPS = 2 * 2 * B * K * G * H + 3 * 2 * B * G * H * E
 
@@ -58,65 +72,64 @@ def tile_hyperlstmcell_pb_kernel(
 ):
     nc = tc.nc
     with ExitStack() as ctx:
+        ctx.enter_context(tc.manual_schedule())
         const = ctx.enter_context(tc.tile_pool(name="const", bufs=1))
         per_gate = ctx.enter_context(tc.tile_pool(name="per_gate", bufs=2))
         work = ctx.enter_context(tc.tile_pool(name="work", bufs=3))
-        gates = ctx.enter_context(tc.tile_pool(name="gates", bufs=3))
-        small = ctx.enter_context(tc.tile_pool(name="small", bufs=4))
-        stage = ctx.enter_context(tc.tile_pool(name="stage", bufs=4))
-        late = ctx.enter_context(tc.tile_pool(name="late", bufs=B_TILES))
-        psum_one = ctx.enter_context(tc.psum_pool(name="psum_one", bufs=1))
-        psum_two = ctx.enter_context(tc.psum_pool(name="psum_two", bufs=2))
-
-        ident_bf = const.tile([P, P], BF16)
-        make_identity(nc, ident_bf[:])
-        ident_f32 = const.tile([P, P], F32)
-        make_identity(nc, ident_f32[:])
-        one_half = const.tile([P, 1], F32)
-        nc.vector.memset(one_half[:], 0.5)
-        warm = const.tile([P, 1], F32)
-        nc.scalar.activation(out=warm[:], in_=one_half[:], func=ACT.Sigmoid)
+        jobs = ctx.enter_context(tc.tile_pool(name="jobs", bufs=4))
+        small = ctx.enter_context(tc.tile_pool(name="small", bufs=6))
+        psum = ctx.enter_context(tc.psum_pool(name="psum", bufs=1))
 
         planes = const.tile([P, G * H], U8, align_bytes=64)
         nc.vector.memset(planes[:].bitcast(I32), 0)
+        one_half = const.tile([P, 1], F32)
+        nc.vector.memset(one_half[:], 0.5)
+        norm_rows = const.tile([P, P], BF16)
+        nc.vector.memset(norm_rows[:], 0.0)
+        warm = const.tile([P, 1], F32)
+        nc.scalar.activation(out=warm[:], in_=one_half[:], func=ACT.Sigmoid)
+        ident_f32 = const.tile([P, P], F32)
+        make_identity(nc, ident_f32[:])
+        ident_bf = const.tile([P, P], BF16)
+        make_identity(nc, ident_bf[:])
 
-        act_codes = const.tile([P, 2, B_TILES, PASSES, P], U32, align_bytes=64)
-        act_scales = const.tile([P, 2, B_TILES, PASSES, P], U8, align_bytes=64)
-        emb_t = [const.tile([P, G, B], BF16, name="emb_t%d" % i) for i in range(3)]
-        c_sb = const.tile([P, B_TILES, H], BF16)
-
+        act_raw = const.tile([P, 2, B_TILES, K], BF16)
         for bt in range(B_TILES):
-            rows = slice(bt * P, (bt + 1) * P)
             for operand, source in enumerate((x, h)):
-                raw = stage.tile([P, K], BF16)
-                nc.sync.dma_start(out=raw[:], in_=source[rows, :])
-                words = raw[:].bitcast(F32)
-                flipped = psum_two.tile([P, PASSES, 2, P], F32, tag="flip")
-                for g in range(PASSES):
-                    for u in range(2):
-                        nc.tensor.transpose(
-                            flipped[:, g, u, :],
-                            words[:, 256 * g + u : 256 * (g + 1) : 2],
-                            ident_f32[:],
-                        )
-                grouped = stage.tile([P, PASSES * P * 4], BF16, align_bytes=64)
-                nc.vector.tensor_copy(
-                    out=grouped[:].bitcast(F32).rearrange("p (g b u) -> p g b u", g=PASSES, u=2),
-                    in_=flipped[:].rearrange("p g u b -> p g b u"),
-                )
-                nc.vector.quantize_mx(
-                    out=act_codes[:, operand, bt].rearrange("p g b -> p (g b)").bitcast(FP8X4),
-                    scales=act_scales[:, operand, bt].rearrange("p g b -> p (g b)"),
-                    in_=grouped[:],
-                )
-            for i, source in enumerate((emb_x, emb_h, emb_b)):
-                emb_raw = stage.tile([P, G, E], BF16)
-                nc.sync.dma_start(out=emb_raw[:], in_=source[rows])
-                emb_flip = psum_two.tile([P, G, P], BF16, tag="flip")
-                for gate in range(G):
-                    nc.tensor.transpose(emb_flip[:, gate, :], emb_raw[:, gate, :], ident_bf[:])
-                nc.scalar.copy(out=emb_t[i][:, :, rows], in_=emb_flip[:])
+                nc.sync.dma_start(out=act_raw[:, operand, bt, :], in_=source[bt * P : (bt + 1) * P, :])
+        emb_raw = const.tile([P, 3, B_TILES, G * E], BF16)
+        for i, source in enumerate((emb_x, emb_h, emb_b)):
+            nc.sync.dma_start(out=emb_raw[:, i], in_=source.rearrange("(t p) g e -> p t (g e)", p=P))
 
+        w_words = [None] * G
+        ws_raw = [None] * G
+        ws_t = [[None] * 3 for position in range(G)]
+        bias_row = [None] * G
+
+        def load_gate(position):
+            gate = GATE_ORDER[position]
+            raws = []
+            for i, source in enumerate((Wsx, Wsh, Wsb)):
+                raw = per_gate.tile([P, UNIT_BLOCKS, E], BF16, name="ws_raw%d" % i)
+                nc.sync.dma_start(out=raw[:], in_=source[gate].rearrange("(j p) e -> p j e", p=P))
+                raws.append(raw)
+            ws_raw[position] = raws
+            row = per_gate.tile([P, H], BF16, name="bias_row")
+            nc.scalar.dma_start(out=row[:], in_=bias[gate * H : (gate + 1) * H].partition_broadcast(P))
+            bias_row[position] = row
+            words = per_gate.tile([P, 2, PASSES, H], U32, name="w_words", align_bytes=64)
+            for operand, source in enumerate((Wih_words, Whh_words)):
+                for g in range(PASSES):
+                    nc.sync.dma_start(
+                        out=words[:, operand, g, :].bitcast(I32),
+                        in_=source[g, :, gate * H : (gate + 1) * H, :].rearrange("p n t -> p (n t)").bitcast(I32),
+                    )
+            w_words[position] = words
+
+        nc.sync.dma_start(out=norm_rows[0 : G * UNIT_BLOCKS, :], in_=ln_gamma.rearrange("g (j p) -> (g j) p", p=P))
+        nc.sync.dma_start(
+            out=norm_rows[G * UNIT_BLOCKS : 2 * G * UNIT_BLOCKS, :], in_=ln_beta.rearrange("g (j p) -> (g j) p", p=P)
+        )
         for operand, source in enumerate((Wih_scales, Whh_scales)):
             for quad in range(4):
                 first = 32 * quad + 8 * operand
@@ -124,28 +137,159 @@ def tile_hyperlstmcell_pb_kernel(
                     out=planes[first : first + 8, :].bitcast(I32),
                     in_=source[:, 4 * quad : 4 * quad + 4, :].bitcast(I32),
                 )
+        load_gate(0)
+        c_raw = const.tile([P, B_TILES, H], BF16)
+        nc.sync.dma_start(out=c_raw[:], in_=c.rearrange("(t p) n -> p t n", p=P))
+        load_gate(1)
 
-        bias_bc = const.tile([P, G, H], BF16)
-        gamma_bc = const.tile([P, G, H], BF16)
-        beta_bc = const.tile([P, G, H], BF16)
-        nc.scalar.dma_start(out=bias_bc[:].rearrange("p g n -> p (g n)"), in_=bias.partition_broadcast(P))
-        nc.scalar.dma_start(
-            out=gamma_bc[:].rearrange("p g n -> p (g n)"),
-            in_=ln_gamma.rearrange("g n -> (g n)").partition_broadcast(P),
-        )
-        nc.scalar.dma_start(
-            out=beta_bc[:].rearrange("p g n -> p (g n)"),
-            in_=ln_beta.rearrange("g n -> (g n)").partition_broadcast(P),
-        )
-        gamma_c_bc = const.tile([P, H], BF16)
-        beta_c_bc = const.tile([P, H], BF16)
-        nc.scalar.dma_start(out=gamma_c_bc[:], in_=lnc_gamma.partition_broadcast(P))
-        nc.scalar.dma_start(out=beta_c_bc[:], in_=lnc_beta.partition_broadcast(P))
-        nc.sync.dma_start(out=c_sb[:], in_=c.rearrange("(t p) n -> p t n", p=P))
+        late_rows = {}
 
-        def norm_scalars(sum_parts, sum_squares):
+        def load_late_rows():
+            sources = (
+                ("gamma_o", ln_gamma[GATE_O]),
+                ("beta_o", ln_beta[GATE_O]),
+                ("gamma_c", lnc_gamma),
+                ("beta_c", lnc_beta),
+            )
+            for name, source in sources:
+                row = const.tile([P, H], BF16, name=name)
+                nc.scalar.dma_start(out=row[:], in_=source.partition_broadcast(P))
+                late_rows[name] = row
+
+        act_codes = const.tile([P, 2, B_TILES, PASSES, P], U32, align_bytes=64)
+        act_scales = const.tile([P, 2, B_TILES, PASSES, P], U8, align_bytes=64)
+        emb_t = [const.tile([P, G, B], BF16, name="emb_t%d" % i) for i in range(3)]
+        for bt in range(B_TILES):
+            grouped = []
+            for operand, tag in enumerate(("xh", "hh")):
+                words = act_raw[:, operand, bt, :].bitcast(F32)
+                flipped = psum.tile([P, PASSES, 2, P], F32, tag=tag)
+                for g in range(PASSES):
+                    for u in range(2):
+                        nc.tensor.transpose(
+                            flipped[:, g, u, :], words[:, 256 * g + u : 256 * (g + 1) : 2], ident_f32[:]
+                        )
+                together = work.tile([P, PASSES * P * 4], BF16, name="grouped%d" % operand, bufs=2, align_bytes=64)
+                nc.vector.tensor_copy(
+                    out=together[:].bitcast(F32).rearrange("p (g b u) -> p g b u", g=PASSES, u=2),
+                    in_=flipped[:].rearrange("p g u b -> p g b u"),
+                )
+                grouped.append(together)
+            for operand in range(2):
+                nc.vector.quantize_mx(
+                    out=act_codes[:, operand, bt].rearrange("p g b -> p (g b)").bitcast(FP8X4),
+                    scales=act_scales[:, operand, bt].rearrange("p g b -> p (g b)"),
+                    in_=grouped[operand][:],
+                )
+        for bt in range(B_TILES):
+            rows = slice(bt * P, (bt + 1) * P)
+            for i, tag in enumerate(("zx", "zh", "zb")):
+                emb_flip = psum.tile([P, G, P], BF16, tag=tag)
+                for gate in range(G):
+                    nc.tensor.transpose(emb_flip[:, gate, :], emb_raw[:, i, bt, gate * E : (gate + 1) * E], ident_bf[:])
+                nc.scalar.copy(out=emb_t[i][:, :, rows], in_=emb_flip[:])
+
+        norm_flip = psum.tile([P, P], BF16, tag="side")
+        nc.tensor.transpose(norm_flip[:], norm_rows[:], ident_bf[:])
+        norm_cols = const.tile([P, 2 * G * UNIT_BLOCKS], F32)
+        nc.vector.tensor_copy(out=norm_cols[:], in_=norm_flip[:, 0 : 2 * G * UNIT_BLOCKS])
+
+        def flip_ws(position, i):
+            ws_flip = psum.tile([P, UNIT_BLOCKS, P], BF16, tag="side")
+            for j in range(UNIT_BLOCKS):
+                nc.tensor.transpose(ws_flip[:, j, :], ws_raw[position][i][:, j, :], ident_bf[:])
+            flat = per_gate.tile([P, H], BF16, name="ws_t%d" % i)
+            nc.scalar.copy(out=flat[:], in_=ws_flip[:].rearrange("p j n -> p (j n)"))
+            ws_t[position][i] = flat
+
+        for i in range(3):
+            flip_ws(0, i)
+
+        c_t = const.tile([P, B_TILES, UNIT_BLOCKS, P], BF16)
+
+        def flip_c(bt):
+            c_flip = psum.tile([P, UNIT_BLOCKS, P], BF16, tag="side")
+            for j in range(UNIT_BLOCKS):
+                nc.tensor.transpose(c_flip[:, j, :], c_raw[:, bt, j * P : (j + 1) * P], ident_bf[:])
+            nc.scalar.copy(out=c_t[:, bt], in_=c_flip[:])
+
+        pre = [None] * JOBS
+        sum_parts = [None] * JOBS
+        mean_of = {}
+        std_of = {}
+        rstd_of = {}
+        flipped_pre = [None] * JOBS
+        flipped_act = [None] * JOBS
+        state = [None] * B_TILES
+        cell_banks = [None] * B_TILES
+        cell = [None] * B_TILES
+        tanh_c = [None] * B_TILES
+
+        def gate_of(job):
+            return GATE_ORDER[job // B_TILES]
+
+        def front(k):
+            job, half = divmod(k, HALVES)
+            position, bt = divmod(job, B_TILES)
+            gate = GATE_ORDER[position]
+            rows = slice(bt * P, (bt + 1) * P)
+            cols = slice(half * N_TILE, (half + 1) * N_TILE)
+            all_cols = slice(gate * H + half * N_TILE, gate * H + (half + 1) * N_TILE)
+            z_ps = []
+            for i, tag in ((2, "zb"), (0, "zx"), (1, "zh")):
+                z = psum.tile([P, N_TILE], F32, tag=tag)
+                nc.tensor.matmul(
+                    out=z[:], lhsT=emb_t[i][:, gate, rows], rhs=ws_t[position][i][:, cols], start=True, stop=True
+                )
+                z_ps.append(z)
+            mx_ps = []
+            for operand, tag in enumerate(("xh", "hh")):
+                acc = psum.tile([P, N_TILE], F32, tag=tag)
+                for g in range(PASSES):
+                    first = 8 * operand + 4 * g
+                    nc.tensor.matmul_mx(
+                        out=acc[:],
+                        lhsT=act_codes[:, operand, bt, g, :].bitcast(FP8X4),
+                        lhsT_scale=act_scales[:, operand, bt, g, :],
+                        rhs=w_words[position][:, operand, g, cols].bitcast(FP8X4),
+                        rhs_scale=planes[first:P, all_cols],
+                        start=(g == 0),
+                        stop=(g == PASSES - 1),
+                    )
+                mx_ps.append(acc)
+
+            if half == 0:
+                pre[job] = jobs.tile([P, H], F32, name="pre")
+                sum_parts[job] = small.tile([P, 3 * HALVES], F32, name="sum_parts")
+            parts = sum_parts[job]
+            shift = work.tile([P, N_TILE], F32)
+            nc.vector.scalar_tensor_tensor(
+                out=shift[:], in0=z_ps[0][:], scalar=1.0, in1=bias_row[position][:, cols],
+                op0=ALU.mult, op1=ALU.add, accum_out=parts[:, 3 * half : 3 * half + 1],
+            )
+            zx_sb = work.tile([P, N_TILE], F32)
+            nc.scalar.copy(out=zx_sb[:], in_=z_ps[1][:])
+            zh_sb = work.tile([P, N_TILE], F32)
+            nc.scalar.copy(out=zh_sb[:], in_=z_ps[2][:])
+            term_x = work.tile([P, N_TILE], F32)
+            nc.vector.scalar_tensor_tensor(
+                out=term_x[:], in0=mx_ps[0][:], scalar=1.0, in1=zx_sb[:],
+                op0=ALU.mult, op1=ALU.mult, accum_out=parts[:, 3 * half + 1 : 3 * half + 2],
+            )
+            term_h = work.tile([P, N_TILE], F32)
+            nc.vector.scalar_tensor_tensor(
+                out=term_h[:], in0=mx_ps[1][:], scalar=1.0, in1=zh_sb[:],
+                op0=ALU.mult, op1=ALU.mult, accum_out=parts[:, 3 * half + 2 : 3 * half + 3],
+            )
+            nc.gpsimd.tensor_tensor(out=term_x[:], in0=term_x[:], in1=term_h[:], op=ALU.add)
+            nc.gpsimd.tensor_tensor(out=pre[job][:, cols], in0=term_x[:], in1=shift[:], op=ALU.add)
+
+        def start_norm(key, parts, values):
+            squares = work.tile([P, H], BF16, bufs=2)
+            sum_squares = small.tile([P, 1], F32)
+            nc.scalar.activation(out=squares[:], in_=values, func=ACT.Square, accum_out=sum_squares[:])
             total = small.tile([P, 1], F32)
-            nc.vector.tensor_tensor(out=total[:], in0=sum_parts[:, 0:1], in1=sum_parts[:, 1:2], op=ALU.add)
+            nc.vector.tensor_reduce(out=total[:], in_=parts, axis=AXIS.X, op=ALU.add)
             mean = small.tile([P, 1], F32)
             nc.vector.tensor_scalar(out=mean[:], in0=total[:], scalar1=1.0 / H, scalar2=None, op0=ALU.mult)
             spread = small.tile([P, 1], F32)
@@ -158,130 +302,155 @@ def tile_hyperlstmcell_pb_kernel(
             )
             std = small.tile([P, 1], F32)
             nc.gpsimd.tensor_tensor(out=std[:], in0=variance[:], in1=one_half[:], op=ALU.pow)
+            mean_of[key] = mean
+            std_of[key] = std
+
+        def finish_norm(key):
+            padded = small.tile([P, 1], F32)
+            nc.vector.tensor_scalar(out=padded[:], in0=std_of[key][:], scalar1=EPS, scalar2=None, op0=ALU.add)
             rstd = small.tile([P, 1], F32)
-            nc.vector.tensor_scalar(out=rstd[:], in0=std[:], scalar1=EPS, scalar2=None, op0=ALU.add)
-            nc.vector.reciprocal(out=rstd[:], in_=rstd[:])
-            return mean, rstd
+            nc.vector.reciprocal(out=rstd[:], in_=padded[:])
+            rstd_of[key] = rstd
 
-        def sum_of_squares(values):
-            squares = work.tile([P, H], BF16, bufs=2)
-            sum_squares = small.tile([P, 1], F32)
-            nc.scalar.activation(out=squares[:], in_=values, func=ACT.Square, accum_out=sum_squares[:])
-            return sum_squares
-
-        def scale_and_shift(values, mean, rstd, gamma_row, beta_row):
+        def scale_and_shift(key, values, gamma_row, beta_row):
             nc.vector.scalar_tensor_tensor(
-                out=values, in0=values, scalar=mean[:, 0:1], in1=gamma_row, op0=ALU.subtract, op1=ALU.mult
+                out=values, in0=values, scalar=mean_of[key][:, 0:1], in1=gamma_row[:], op0=ALU.subtract, op1=ALU.mult
             )
             nc.vector.scalar_tensor_tensor(
-                out=values, in0=values, scalar=rstd[:, 0:1], in1=beta_row, op0=ALU.mult, op1=ALU.add
+                out=values, in0=values, scalar=rstd_of[key][:, 0:1], in1=beta_row[:], op0=ALU.mult, op1=ALU.add
             )
 
-        product_ig = [None] * B_TILES
-        tanh_c = [None] * B_TILES
+        def normalise(job):
+            finish_norm(job)
+            if gate_of(job) == GATE_O:
+                scale_and_shift(job, pre[job][:], late_rows["gamma_o"], late_rows["beta_o"])
+            else:
+                nc.vector.tensor_scalar(
+                    out=pre[job][:], in0=pre[job][:], scalar1=mean_of[job][:, 0:1], scalar2=rstd_of[job][:, 0:1],
+                    op0=ALU.subtract, op1=ALU.mult,
+                )
 
-        for gate in GATE_ORDER:
-            w_words = per_gate.tile([P, 2, PASSES, H], U32, align_bytes=64)
-            for operand, source in enumerate((Wih_words, Whh_words)):
-                for g in range(PASSES):
-                    nc.sync.dma_start(
-                        out=w_words[:, operand, g, :].bitcast(I32),
-                        in_=source[g, :, gate * H : (gate + 1) * H, :].rearrange("p n t -> p (n t)").bitcast(I32),
-                    )
-            ws_t = []
-            for i, source in enumerate((Wsx, Wsh, Wsb)):
-                ws_raw = per_gate.tile([P, UNIT_BLOCKS, E], BF16, name="ws_raw%d" % i)
-                nc.sync.dma_start(out=ws_raw[:], in_=source[gate].rearrange("(j p) e -> p j e", p=P))
-                ws_flip = psum_two.tile([P, UNIT_BLOCKS, P], BF16, tag="flip")
-                for j in range(UNIT_BLOCKS):
-                    nc.tensor.transpose(ws_flip[:, j, :], ws_raw[:, j, :], ident_bf[:])
-                flat = per_gate.tile([P, H], BF16, name="ws_t%d" % i)
-                nc.scalar.copy(out=flat[:], in_=ws_flip[:].rearrange("p j n -> p (j n)"))
-                ws_t.append(flat)
+        def flip(job):
+            if gate_of(job) == GATE_O:
+                nc.scalar.activation(out=pre[job][:], in_=pre[job][:], func=ACT.Sigmoid)
+                return
+            banks = []
+            for half in range(HALVES):
+                bank = psum.tile([P, BANK_BLOCKS, P], F32, tag="flip", bufs=2)
+                for j in range(BANK_BLOCKS):
+                    block = half * BANK_BLOCKS + j
+                    nc.tensor.transpose(bank[:, j, :], pre[job][:, block * P : (block + 1) * P], ident_f32[:])
+                banks.append(bank)
+            flipped_pre[job] = banks
 
-            for bt in range(B_TILES):
-                rows = slice(bt * P, (bt + 1) * P)
-                if gate == GATE_I:
-                    pre = late.tile([P, H], F32, tag="product_ig")
-                else:
-                    pre = gates.tile([P, H], F32, tag="pre")
-                sum_parts = small.tile([P, HALVES], F32)
-                for half in range(HALVES):
-                    cols = slice(half * N_TILE, (half + 1) * N_TILE)
-                    all_cols = slice(gate * H + half * N_TILE, gate * H + (half + 1) * N_TILE)
-                    z_ps = []
-                    for i, tag in enumerate(("zx", "zh")):
-                        z = psum_one.tile([P, N_TILE], F32, tag=tag)
-                        nc.tensor.matmul(out=z[:], lhsT=emb_t[i][:, gate, rows], rhs=ws_t[i][:, cols], start=True, stop=True)
-                        z_ps.append(z)
-                    zb_ps = psum_two.tile([P, N_TILE], F32, tag="zb")
-                    nc.tensor.matmul(out=zb_ps[:], lhsT=emb_t[2][:, gate, rows], rhs=ws_t[2][:, cols], start=True, stop=True)
-                    mx_ps = []
-                    for operand, tag in enumerate(("xh", "hh")):
-                        acc = psum_one.tile([P, N_TILE], F32, tag=tag)
-                        for g in range(PASSES):
-                            first = 8 * operand + 4 * g
-                            nc.tensor.matmul_mx(
-                                out=acc[:],
-                                lhsT=act_codes[:, operand, bt, g, :].bitcast(FP8X4),
-                                lhsT_scale=act_scales[:, operand, bt, g, :],
-                                rhs=w_words[:, operand, g, cols].bitcast(FP8X4),
-                                rhs_scale=planes[first:P, all_cols],
-                                start=(g == 0),
-                                stop=(g == PASSES - 1),
-                            )
-                        mx_ps.append(acc)
+        def activate(job):
+            gate = gate_of(job)
+            bt = job % B_TILES
+            if gate == GATE_O:
+                nc.vector.tensor_tensor(out=tanh_c[bt][:], in0=tanh_c[bt][:], in1=pre[job][:], op=ALU.mult)
+                nc.sync.dma_start(out=out_0[bt * P : (bt + 1) * P, :], in_=tanh_c[bt][:])
+                return
+            if gate == GATE_I:
+                target = jobs.tile([P, UNIT_BLOCKS, P], F32, name="state")
+                state[bt] = target
+            else:
+                target = jobs.tile([P, UNIT_BLOCKS, P], F32, name="flipped_act", bufs=2)
+                flipped_act[job] = target
+            func = ACT.Tanh if gate == GATE_G else ACT.Sigmoid
+            for block in range(UNIT_BLOCKS):
+                column = gate * UNIT_BLOCKS + block
+                nc.scalar.activation(
+                    out=target[:, block, :],
+                    in_=flipped_pre[job][block // BANK_BLOCKS][:, block % BANK_BLOCKS, :],
+                    func=func,
+                    scale=norm_cols[:, column : column + 1],
+                    bias=norm_cols[:, G * UNIT_BLOCKS + column : G * UNIT_BLOCKS + column + 1],
+                )
 
-                    zx_sb = work.tile([P, N_TILE], F32)
-                    nc.scalar.copy(out=zx_sb[:], in_=z_ps[0][:])
-                    term_x = work.tile([P, N_TILE], F32)
-                    nc.vector.tensor_tensor(out=term_x[:], in0=mx_ps[0][:], in1=zx_sb[:], op=ALU.mult)
-                    nc.gpsimd.tensor_tensor(out=term_x[:], in0=term_x[:], in1=bias_bc[:, gate, cols], op=ALU.add)
-                    zh_sb = work.tile([P, N_TILE], F32)
-                    nc.scalar.copy(out=zh_sb[:], in_=z_ps[1][:])
-                    term_h = work.tile([P, N_TILE], F32)
-                    nc.vector.tensor_tensor(out=term_h[:], in0=mx_ps[1][:], in1=zh_sb[:], op=ALU.mult)
-                    nc.gpsimd.tensor_tensor(out=term_x[:], in0=term_x[:], in1=term_h[:], op=ALU.add)
-                    nc.vector.scalar_tensor_tensor(
-                        out=pre[:, cols],
-                        in0=zb_ps[:],
-                        scalar=1.0,
-                        in1=term_x[:],
-                        op0=ALU.mult,
-                        op1=ALU.add,
-                        accum_out=sum_parts[:, half : half + 1],
-                    )
+        def cell_step(job):
+            gate = gate_of(job)
+            bt = job % B_TILES
+            if gate == GATE_G:
+                nc.vector.tensor_tensor(out=state[bt][:], in0=state[bt][:], in1=flipped_act[job][:], op=ALU.mult)
+            if gate == GATE_F:
+                nc.vector.tensor_tensor(out=flipped_act[job][:], in0=flipped_act[job][:], in1=c_t[:, bt], op=ALU.mult)
+                nc.vector.tensor_tensor(out=state[bt][:], in0=state[bt][:], in1=flipped_act[job][:], op=ALU.add)
 
-                mean, rstd = norm_scalars(sum_parts, sum_of_squares(pre[:]))
-                scale_and_shift(pre[:], mean, rstd, gamma_bc[:, gate, :], beta_bc[:, gate, :])
-                func = ACT.Tanh if gate == GATE_G else ACT.Sigmoid
-                nc.scalar.activation(out=pre[:], in_=pre[:], func=func)
+        def unflip(bt):
+            banks = []
+            for half in range(HALVES):
+                bank = psum.tile([P, BANK_BLOCKS, P], F32, tag="flip", bufs=2)
+                for j in range(BANK_BLOCKS):
+                    nc.tensor.transpose(bank[:, j, :], state[bt][:, half * BANK_BLOCKS + j, :], ident_f32[:])
+                banks.append(bank)
+            cell_banks[bt] = banks
 
-                if gate == GATE_I:
-                    product_ig[bt] = pre
-                elif gate == GATE_G:
-                    nc.gpsimd.tensor_tensor(out=product_ig[bt][:], in0=product_ig[bt][:], in1=pre[:], op=ALU.mult)
-                elif gate == GATE_F:
-                    cell = product_ig[bt]
-                    nc.vector.tensor_tensor(out=pre[:], in0=pre[:], in1=c_sb[:, bt, :], op=ALU.mult)
-                    cell_sums = small.tile([P, HALVES], F32)
-                    for half in range(HALVES):
-                        cols = slice(half * N_TILE, (half + 1) * N_TILE)
-                        nc.vector.scalar_tensor_tensor(
-                            out=cell[:, cols],
-                            in0=cell[:, cols],
-                            scalar=1.0,
-                            in1=pre[:, cols],
-                            op0=ALU.mult,
-                            op1=ALU.add,
-                            accum_out=cell_sums[:, half : half + 1],
-                        )
-                    mean, rstd = norm_scalars(cell_sums, sum_of_squares(cell[:]))
-                    scale_and_shift(cell[:], mean, rstd, gamma_c_bc[:], beta_c_bc[:])
-                    nc.sync.dma_start(out=out_1[rows, :], in_=cell[:])
-                    squashed = late.tile([P, H], F32, tag="tanh_c")
-                    nc.scalar.activation(out=squashed[:], in_=cell[:], func=ACT.Tanh)
-                    tanh_c[bt] = squashed
-                else:
-                    nc.vector.tensor_tensor(out=tanh_c[bt][:], in0=tanh_c[bt][:], in1=pre[:], op=ALU.mult)
-                    nc.sync.dma_start(out=out_0[rows, :], in_=tanh_c[bt][:])
+        def cell_sums(bt):
+            cell[bt] = jobs.tile([P, H], F32, name="cell", bufs=2)
+            parts = small.tile([P, HALVES], F32, name="cell_parts")
+            for half in range(HALVES):
+                nc.scalar.activation(
+                    out=cell[bt][:, half * N_TILE : (half + 1) * N_TILE],
+                    in_=cell_banks[bt][half][:].rearrange("p j n -> p (j n)"),
+                    func=ACT.Identity,
+                    accum_out=parts[:, half : half + 1],
+                )
+            start_norm(("cell", bt), parts[:], cell[bt][:])
+
+        def cell_norm(bt):
+            finish_norm(("cell", bt))
+            scale_and_shift(("cell", bt), cell[bt][:], late_rows["gamma_c"], late_rows["beta_c"])
+            nc.sync.dma_start(out=out_1[bt * P : (bt + 1) * P, :], in_=cell[bt][:])
+
+        def cell_tanh(bt):
+            tanh_c[bt] = jobs.tile([P, H], F32, name="state")
+            nc.scalar.activation(out=tanh_c[bt][:], in_=cell[bt][:], func=ACT.Tanh)
+
+        def job_due(k, lag):
+            job, odd = divmod(k - lag, HALVES)
+            return job if odd == 0 and 0 <= job < JOBS else None
+
+        def forget_job_due(k, lag):
+            job = job_due(k, lag)
+            return job if job is not None and gate_of(job) == GATE_F else None
+
+        slots_a_gate = SLOTS // G
+        for k in range(SLOTS + LAG_CELL_TANH + 1):
+            position, step = divmod(k, slots_a_gate)
+            if k < SLOTS:
+                front(k)
+            if k < B_TILES:
+                flip_c(k)
+            if step == 1 and 1 <= position < G - 1:
+                load_gate(position + 1)
+            if k == slots_a_gate + 1:
+                load_late_rows()
+            if 4 <= step < 7 and position < G - 1:
+                flip_ws(position + 1, step - 4)
+            job = forget_job_due(k, LAG_CELL_TANH)
+            if job is not None:
+                cell_tanh(job % B_TILES)
+            job = forget_job_due(k, LAG_CELL_NORM)
+            if job is not None:
+                cell_norm(job % B_TILES)
+            job = forget_job_due(k, LAG_CELL_SUMS)
+            if job is not None:
+                cell_sums(job % B_TILES)
+            job = job_due(k, LAG_CELL)
+            if job is not None:
+                cell_step(job)
+            job = job_due(k, LAG_ACTIVATE)
+            if job is not None:
+                activate(job)
+            job = forget_job_due(k, LAG_UNFLIP)
+            if job is not None:
+                unflip(job % B_TILES)
+            job = job_due(k, LAG_FLIP)
+            if job is not None:
+                flip(job)
+            job = job_due(k, LAG_NORMALISE)
+            if job is not None:
+                normalise(job)
+            job = job_due(k, LAG_SUMS)
+            if job is not None:
+                start_norm(job, sum_parts[job][:], pre[job][:])

@@ -281,8 +281,8 @@ def tile_hyperlstmcell_pb_kernel(
                 out=term_h[:], in0=mx_ps[1][:], scalar=1.0, in1=zh_sb[:],
                 op0=ALU.mult, op1=ALU.mult, accum_out=parts[:, 3 * half + 2 : 3 * half + 3],
             )
-            nc.gpsimd.tensor_tensor(out=term_x[:], in0=term_x[:], in1=term_h[:], op=ALU.add)
-            nc.gpsimd.tensor_tensor(out=pre[job][:, cols], in0=term_x[:], in1=shift[:], op=ALU.add)
+            nc.vector.tensor_tensor(out=term_x[:], in0=term_x[:], in1=term_h[:], op=ALU.add)
+            nc.vector.tensor_tensor(out=pre[job][:, cols], in0=term_x[:], in1=shift[:], op=ALU.add)
 
         def start_norm(key, parts, values):
             squares = work.tile([P, H], BF16, bufs=2)

@@ -34,15 +34,27 @@ GATE_ORDER = (GATE_I, GATE_G, GATE_F, GATE_O)
 JOBS = G * B_TILES
 SLOTS = JOBS * HALVES
 
-LAG_SUMS = 3
-LAG_NORMALISE = 4
-LAG_FLIP = 5
-LAG_ACTIVATE = 6
-LAG_CELL = 7
-LAG_UNFLIP = 8
-LAG_CELL_SUMS = 9
-LAG_CELL_NORM = 10
-LAG_CELL_TANH = 11
+LAG_SQUARE = 2
+LAG_TOTAL = 2
+LAG_SPREAD = 3
+LAG_ROOT = 4
+LAG_RSTD = 5
+LAG_NORMALISE = 5
+LAG_FLIP = 6
+LAG_ACTIVATE = 7
+LAG_CELL = 8
+LAG_RETURN = 8
+LAG_OUTPUT = 9
+LAG_UNFLIP = 9
+LAG_CELL_OUT = 10
+LAG_CELL_SQUARE = 11
+LAG_CELL_TOTAL = 12
+LAG_CELL_ROOT = 13
+LAG_CELL_RSTD = 14
+LAG_CELL_NORMALISE = 14
+LAG_CELL_SHIFT = 15
+LAG_CELL_TANH = 16
+LAST_LAG = LAG_CELL_TANH + 1
 
 FLOPS = 2 * 2 * B * K * G * H + 3 * 2 * B * G * H * E
 
@@ -77,13 +89,18 @@ def tile_hyperlstmcell_pb_kernel(
         per_gate = ctx.enter_context(tc.tile_pool(name="per_gate", bufs=2))
         work = ctx.enter_context(tc.tile_pool(name="work", bufs=3))
         jobs = ctx.enter_context(tc.tile_pool(name="jobs", bufs=4))
-        small = ctx.enter_context(tc.tile_pool(name="small", bufs=6))
+        small = ctx.enter_context(tc.tile_pool(name="small", bufs=8))
         psum = ctx.enter_context(tc.psum_pool(name="psum", bufs=1))
+
+        def flip_bank(shape, dtype):
+            return psum.tile(shape, dtype, name="flip", bufs=3)
 
         planes = const.tile([P, G * H], U8, align_bytes=64)
         nc.vector.memset(planes[:].bitcast(I32), 0)
         one_half = const.tile([P, 1], F32)
         nc.vector.memset(one_half[:], 0.5)
+        rows = const.tile([P, N_TILE], BF16)
+        nc.vector.memset(rows[:], 0.0)
         norm_rows = const.tile([P, P], BF16)
         nc.vector.memset(norm_rows[:], 0.0)
         warm = const.tile([P, 1], F32)
@@ -93,30 +110,33 @@ def tile_hyperlstmcell_pb_kernel(
         ident_bf = const.tile([P, P], BF16)
         make_identity(nc, ident_bf[:])
 
-        act_raw = const.tile([P, 2, B_TILES, K], BF16)
-        for bt in range(B_TILES):
+        act_raw = [None] * B_TILES
+        emb_raw = [None] * B_TILES
+
+        def load_samples(bt):
+            act_raw[bt] = jobs.tile([P, 2, K], BF16, name="cell")
+            emb_raw[bt] = jobs.tile([P, 3, G * E], BF16, name="state")
             for operand, source in enumerate((x, h)):
-                nc.sync.dma_start(out=act_raw[:, operand, bt, :], in_=source[bt * P : (bt + 1) * P, :])
-        emb_raw = const.tile([P, 3, B_TILES, G * E], BF16)
-        for i, source in enumerate((emb_x, emb_h, emb_b)):
-            nc.sync.dma_start(out=emb_raw[:, i], in_=source.rearrange("(t p) g e -> p t (g e)", p=P))
+                nc.sync.dma_start(out=act_raw[bt][:, operand, :], in_=source[bt * P : (bt + 1) * P, :])
+            for i, source in enumerate((emb_x, emb_h, emb_b)):
+                nc.sync.dma_start(
+                    out=emb_raw[bt][:, i, :], in_=source[bt * P : (bt + 1) * P].rearrange("p g e -> p (g e)")
+                )
 
         w_words = [None] * G
         ws_raw = [None] * G
         ws_t = [[None] * 3 for position in range(G)]
-        bias_row = [None] * G
 
-        def load_gate(position):
-            gate = GATE_ORDER[position]
+        def load_ws(position):
             raws = []
             for i, source in enumerate((Wsx, Wsh, Wsb)):
                 raw = per_gate.tile([P, UNIT_BLOCKS, E], BF16, name="ws_raw%d" % i)
-                nc.sync.dma_start(out=raw[:], in_=source[gate].rearrange("(j p) e -> p j e", p=P))
+                nc.sync.dma_start(out=raw[:], in_=source[GATE_ORDER[position]].rearrange("(j p) e -> p j e", p=P))
                 raws.append(raw)
             ws_raw[position] = raws
-            row = per_gate.tile([P, H], BF16, name="bias_row")
-            nc.scalar.dma_start(out=row[:], in_=bias[gate * H : (gate + 1) * H].partition_broadcast(P))
-            bias_row[position] = row
+
+        def load_words(position):
+            gate = GATE_ORDER[position]
             words = per_gate.tile([P, 2, PASSES, H], U32, name="w_words", align_bytes=64)
             for operand, source in enumerate((Wih_words, Whh_words)):
                 for g in range(PASSES):
@@ -126,10 +146,20 @@ def tile_hyperlstmcell_pb_kernel(
                     )
             w_words[position] = words
 
-        nc.sync.dma_start(out=norm_rows[0 : G * UNIT_BLOCKS, :], in_=ln_gamma.rearrange("g (j p) -> (g j) p", p=P))
-        nc.sync.dma_start(
-            out=norm_rows[G * UNIT_BLOCKS : 2 * G * UNIT_BLOCKS, :], in_=ln_beta.rearrange("g (j p) -> (g j) p", p=P)
-        )
+        row_sources = (bias, lnc_gamma, lnc_beta)
+        first = 0
+        for source in row_sources:
+            count = source.shape[0] // N_TILE
+            nc.gpsimd.dma_start(out=rows[first : first + count, :], in_=source.rearrange("(r n) -> r n", n=N_TILE))
+            first += count
+        for i, source in enumerate((ln_gamma, ln_beta)):
+            nc.gpsimd.dma_start(
+                out=norm_rows[i * G * UNIT_BLOCKS : (i + 1) * G * UNIT_BLOCKS, :],
+                in_=source.rearrange("g (j p) -> (g j) p", p=P),
+            )
+
+        load_samples(0)
+        load_ws(0)
         for operand, source in enumerate((Wih_scales, Whh_scales)):
             for quad in range(4):
                 first = 32 * quad + 8 * operand
@@ -137,39 +167,29 @@ def tile_hyperlstmcell_pb_kernel(
                     out=planes[first : first + 8, :].bitcast(I32),
                     in_=source[:, 4 * quad : 4 * quad + 4, :].bitcast(I32),
                 )
-        load_gate(0)
+        load_words(0)
+        for bt in range(1, B_TILES):
+            load_samples(bt)
+        load_ws(1)
+        load_words(1)
         c_raw = const.tile([P, B_TILES, H], BF16)
         nc.sync.dma_start(out=c_raw[:], in_=c.rearrange("(t p) n -> p t n", p=P))
-        load_gate(1)
-
-        late_rows = {}
-
-        def load_late_rows():
-            sources = (
-                ("gamma_o", ln_gamma[GATE_O]),
-                ("beta_o", ln_beta[GATE_O]),
-                ("gamma_c", lnc_gamma),
-                ("beta_c", lnc_beta),
-            )
-            for name, source in sources:
-                row = const.tile([P, H], BF16, name=name)
-                nc.scalar.dma_start(out=row[:], in_=source.partition_broadcast(P))
-                late_rows[name] = row
 
         act_codes = const.tile([P, 2, B_TILES, PASSES, P], U32, align_bytes=64)
         act_scales = const.tile([P, 2, B_TILES, PASSES, P], U8, align_bytes=64)
         emb_t = [const.tile([P, G, B], BF16, name="emb_t%d" % i) for i in range(3)]
-        for bt in range(B_TILES):
+
+        def prepare_samples(bt):
             grouped = []
-            for operand, tag in enumerate(("xh", "hh")):
-                words = act_raw[:, operand, bt, :].bitcast(F32)
-                flipped = psum.tile([P, PASSES, 2, P], F32, tag=tag)
+            for operand in range(2):
+                words = act_raw[bt][:, operand, :].bitcast(F32)
+                flipped = flip_bank([P, PASSES, 2, P], F32)
                 for g in range(PASSES):
                     for u in range(2):
                         nc.tensor.transpose(
                             flipped[:, g, u, :], words[:, 256 * g + u : 256 * (g + 1) : 2], ident_f32[:]
                         )
-                together = work.tile([P, PASSES * P * 4], BF16, name="grouped%d" % operand, bufs=2, align_bytes=64)
+                together = work.tile([P, PASSES * P * 4], BF16, name="grouped%d" % operand, bufs=1, align_bytes=64)
                 nc.vector.tensor_copy(
                     out=together[:].bitcast(F32).rearrange("p (g b u) -> p g b u", g=PASSES, u=2),
                     in_=flipped[:].rearrange("p g u b -> p g b u"),
@@ -181,276 +201,382 @@ def tile_hyperlstmcell_pb_kernel(
                     scales=act_scales[:, operand, bt].rearrange("p g b -> p (g b)"),
                     in_=grouped[operand][:],
                 )
-        for bt in range(B_TILES):
-            rows = slice(bt * P, (bt + 1) * P)
-            for i, tag in enumerate(("zx", "zh", "zb")):
-                emb_flip = psum.tile([P, G, P], BF16, tag=tag)
+            for i in range(3):
+                emb_flip = flip_bank([P, G, P], BF16)
                 for gate in range(G):
-                    nc.tensor.transpose(emb_flip[:, gate, :], emb_raw[:, i, bt, gate * E : (gate + 1) * E], ident_bf[:])
-                nc.scalar.copy(out=emb_t[i][:, :, rows], in_=emb_flip[:])
-
-        norm_flip = psum.tile([P, P], BF16, tag="side")
-        nc.tensor.transpose(norm_flip[:], norm_rows[:], ident_bf[:])
-        norm_cols = const.tile([P, 2 * G * UNIT_BLOCKS], F32)
-        nc.vector.tensor_copy(out=norm_cols[:], in_=norm_flip[:, 0 : 2 * G * UNIT_BLOCKS])
+                    nc.tensor.transpose(emb_flip[:, gate, :], emb_raw[bt][:, i, gate * E : (gate + 1) * E], ident_bf[:])
+                nc.scalar.copy(out=emb_t[i][:, :, bt * P : (bt + 1) * P], in_=emb_flip[:])
 
         def flip_ws(position, i):
-            ws_flip = psum.tile([P, UNIT_BLOCKS, P], BF16, tag="side")
+            ws_flip = flip_bank([P, UNIT_BLOCKS, P], BF16)
             for j in range(UNIT_BLOCKS):
                 nc.tensor.transpose(ws_flip[:, j, :], ws_raw[position][i][:, j, :], ident_bf[:])
             flat = per_gate.tile([P, H], BF16, name="ws_t%d" % i)
             nc.scalar.copy(out=flat[:], in_=ws_flip[:].rearrange("p j n -> p (j n)"))
             ws_t[position][i] = flat
 
-        for i in range(3):
-            flip_ws(0, i)
-
         c_t = const.tile([P, B_TILES, UNIT_BLOCKS, P], BF16)
 
         def flip_c(bt):
-            c_flip = psum.tile([P, UNIT_BLOCKS, P], BF16, tag="side")
+            c_flip = flip_bank([P, UNIT_BLOCKS, P], BF16)
             for j in range(UNIT_BLOCKS):
                 nc.tensor.transpose(c_flip[:, j, :], c_raw[:, bt, j * P : (j + 1) * P], ident_bf[:])
             nc.scalar.copy(out=c_t[:, bt], in_=c_flip[:])
 
+        bias_all = const.tile([P, G, H], BF16)
+        gamma_c = const.tile([P, H], BF16)
+        beta_c = const.tile([P, H], BF16)
+        spread_list = []
+        for gate in GATE_ORDER:
+            for half in range(HALVES):
+                spread_list.append((gate * HALVES + half, bias_all[:, gate, half * N_TILE : (half + 1) * N_TILE]))
+        for i, target in enumerate((gamma_c, beta_c)):
+            for half in range(HALVES):
+                spread_list.append(((G + i) * HALVES + half, target[:, half * N_TILE : (half + 1) * N_TILE]))
+
+        def spread_two_rows(first_entry):
+            copies = (nc.scalar.copy, nc.vector.tensor_copy)
+            for entry in range(2):
+                r, target = spread_list[first_entry + entry]
+                repeated = flip_bank([P, N_TILE], F32)
+                nc.tensor.matmul(
+                    out=repeated[:], lhsT=ident_bf[:, r : r + 1].to_broadcast([P, P]), rhs=rows[:], start=True, stop=True
+                )
+                copies[entry](out=target, in_=repeated[:])
+
+        norm_cols = const.tile([P, 2 * G * UNIT_BLOCKS], F32)
+
+        def flip_norm_rows():
+            norm_flip = flip_bank([P, P], BF16)
+            nc.tensor.transpose(norm_flip[:], norm_rows[:], ident_bf[:])
+            nc.vector.tensor_copy(out=norm_cols[:], in_=norm_flip[:, 0 : 2 * G * UNIT_BLOCKS])
+
         pre = [None] * JOBS
-        sum_parts = [None] * JOBS
-        mean_of = {}
-        std_of = {}
-        rstd_of = {}
-        flipped_pre = [None] * JOBS
-        flipped_act = [None] * JOBS
-        state = [None] * B_TILES
-        cell_banks = [None] * B_TILES
-        cell = [None] * B_TILES
-        tanh_c = [None] * B_TILES
+        stats = {}
+        banks = {}
+        terms = {}
 
         def gate_of(job):
             return GATE_ORDER[job // B_TILES]
 
-        def front(k):
+        def columns(half):
+            return slice(half * N_TILE, (half + 1) * N_TILE)
+
+        def matmuls(k):
             job, half = divmod(k, HALVES)
             position, bt = divmod(job, B_TILES)
             gate = GATE_ORDER[position]
-            rows = slice(bt * P, (bt + 1) * P)
-            cols = slice(half * N_TILE, (half + 1) * N_TILE)
-            all_cols = slice(gate * H + half * N_TILE, gate * H + (half + 1) * N_TILE)
-            z_ps = []
+            samples = slice(bt * P, (bt + 1) * P)
             for i, tag in ((2, "zb"), (0, "zx"), (1, "zh")):
-                z = psum.tile([P, N_TILE], F32, tag=tag)
+                z = psum.tile([P, N_TILE], F32, name=tag)
                 nc.tensor.matmul(
-                    out=z[:], lhsT=emb_t[i][:, gate, rows], rhs=ws_t[position][i][:, cols], start=True, stop=True
+                    out=z[:], lhsT=emb_t[i][:, gate, samples], rhs=ws_t[position][i][:, columns(half)],
+                    start=True, stop=True,
                 )
-                z_ps.append(z)
-            mx_ps = []
+                banks[tag] = z
             for operand, tag in enumerate(("xh", "hh")):
-                acc = psum.tile([P, N_TILE], F32, tag=tag)
+                acc = psum.tile([P, N_TILE], F32, name=tag)
                 for g in range(PASSES):
-                    first = 8 * operand + 4 * g
+                    first_row = 8 * operand + 4 * g
                     nc.tensor.matmul_mx(
                         out=acc[:],
                         lhsT=act_codes[:, operand, bt, g, :].bitcast(FP8X4),
                         lhsT_scale=act_scales[:, operand, bt, g, :],
-                        rhs=w_words[position][:, operand, g, cols].bitcast(FP8X4),
-                        rhs_scale=planes[first:P, all_cols],
+                        rhs=w_words[position][:, operand, g, columns(half)].bitcast(FP8X4),
+                        rhs_scale=planes[first_row:P, gate * H + half * N_TILE : gate * H + (half + 1) * N_TILE],
                         start=(g == 0),
                         stop=(g == PASSES - 1),
                     )
-                mx_ps.append(acc)
-
+                banks[tag] = acc
             if half == 0:
                 pre[job] = jobs.tile([P, H], F32, name="pre")
-                sum_parts[job] = small.tile([P, 3 * HALVES], F32, name="sum_parts")
-            parts = sum_parts[job]
-            shift = work.tile([P, N_TILE], F32)
-            nc.vector.scalar_tensor_tensor(
-                out=shift[:], in0=z_ps[0][:], scalar=1.0, in1=bias_row[position][:, cols],
-                op0=ALU.mult, op1=ALU.add, accum_out=parts[:, 3 * half : 3 * half + 1],
-            )
-            zx_sb = work.tile([P, N_TILE], F32)
-            nc.scalar.copy(out=zx_sb[:], in_=z_ps[1][:])
-            zh_sb = work.tile([P, N_TILE], F32)
-            nc.scalar.copy(out=zh_sb[:], in_=z_ps[2][:])
-            term_x = work.tile([P, N_TILE], F32)
-            nc.vector.scalar_tensor_tensor(
-                out=term_x[:], in0=mx_ps[0][:], scalar=1.0, in1=zx_sb[:],
-                op0=ALU.mult, op1=ALU.mult, accum_out=parts[:, 3 * half + 1 : 3 * half + 2],
-            )
-            term_h = work.tile([P, N_TILE], F32)
-            nc.vector.scalar_tensor_tensor(
-                out=term_h[:], in0=mx_ps[1][:], scalar=1.0, in1=zh_sb[:],
-                op0=ALU.mult, op1=ALU.mult, accum_out=parts[:, 3 * half + 2 : 3 * half + 3],
-            )
-            nc.vector.tensor_tensor(out=term_x[:], in0=term_x[:], in1=term_h[:], op=ALU.add)
-            nc.vector.tensor_tensor(out=pre[job][:, cols], in0=term_x[:], in1=shift[:], op=ALU.add)
+                stats[job] = {"parts": small.tile([P, 3 * HALVES], F32, name="parts")}
 
-        def start_norm(key, parts, values):
-            squares = work.tile([P, H], BF16, bufs=2)
-            sum_squares = small.tile([P, 1], F32)
-            nc.scalar.activation(out=squares[:], in_=values, func=ACT.Square, accum_out=sum_squares[:])
-            total = small.tile([P, 1], F32)
-            nc.vector.tensor_reduce(out=total[:], in_=parts, axis=AXIS.X, op=ALU.add)
-            mean = small.tile([P, 1], F32)
-            nc.vector.tensor_scalar(out=mean[:], in0=total[:], scalar1=1.0 / H, scalar2=None, op0=ALU.mult)
-            spread = small.tile([P, 1], F32)
+        def copy_z(k):
+            for tag in ("zx", "zh"):
+                z_sb = work.tile([P, N_TILE], F32, name=tag + "_sb")
+                nc.scalar.copy(out=z_sb[:], in_=banks[tag][:])
+                terms[tag] = z_sb
+
+        def leave_psum(k, part, tag, other, op):
+            job, half = divmod(k, HALVES)
+            column = 3 * half + part
+            term = work.tile([P, N_TILE], F32, name="term_" + tag)
             nc.vector.scalar_tensor_tensor(
-                out=spread[:], in0=total[:], scalar=mean[:, 0:1], in1=sum_squares[:], op0=ALU.mult, op1=ALU.subtract
+                out=term[:], in0=banks[tag][:], scalar=1.0, in1=other, op0=ALU.mult, op1=op,
+                accum_out=stats[job]["parts"][:, column : column + 1],
             )
-            variance = small.tile([P, 1], F32)
+            terms[tag] = term
+
+        def add_terms(k):
+            job, half = divmod(k, HALVES)
+            nc.gpsimd.tensor_tensor(out=terms["xh"][:], in0=terms["xh"][:], in1=terms["hh"][:], op=ALU.add)
+            nc.gpsimd.tensor_tensor(out=pre[job][:, columns(half)], in0=terms["xh"][:], in1=terms["zb"][:], op=ALU.add)
+
+        def square_half(key, values, half):
+            if half == 0:
+                stats[key]["squares"] = small.tile([P, HALVES], F32, name="squares")
+            scratch = work.tile([P, N_TILE], BF16, name="scratch", bufs=2)
+            nc.scalar.activation(
+                out=scratch[:], in_=values[:, columns(half)], func=ACT.Square,
+                accum_out=stats[key]["squares"][:, half : half + 1],
+            )
+
+        def norm_total(key):
+            total = small.tile([P, 1], F32, name="total")
+            nc.vector.tensor_reduce(out=total[:], in_=stats[key]["parts"][:], axis=AXIS.X, op=ALU.add)
+            stats[key]["total"] = total
+
+        def norm_mean(key):
+            minus_mean = small.tile([P, 1], F32, name="minus_mean")
             nc.vector.tensor_scalar(
-                out=variance[:], in0=spread[:], scalar1=-1.0 / (H - 1), scalar2=0.0, op0=ALU.mult, op1=ALU.max
+                out=minus_mean[:], in0=stats[key]["total"][:], scalar1=-1.0 / H, scalar2=None, op0=ALU.mult
             )
-            std = small.tile([P, 1], F32)
-            nc.gpsimd.tensor_tensor(out=std[:], in0=variance[:], in1=one_half[:], op=ALU.pow)
-            mean_of[key] = mean
-            std_of[key] = std
+            stats[key]["minus_mean"] = minus_mean
 
-        def finish_norm(key):
-            padded = small.tile([P, 1], F32)
-            nc.vector.tensor_scalar(out=padded[:], in0=std_of[key][:], scalar1=EPS, scalar2=None, op0=ALU.add)
-            rstd = small.tile([P, 1], F32)
-            nc.vector.reciprocal(out=rstd[:], in_=padded[:])
-            rstd_of[key] = rstd
-
-        def scale_and_shift(key, values, gamma_row, beta_row):
+        def norm_spread(key):
+            spread = small.tile([P, 1], F32, name="spread")
             nc.vector.scalar_tensor_tensor(
-                out=values, in0=values, scalar=mean_of[key][:, 0:1], in1=gamma_row[:], op0=ALU.subtract, op1=ALU.mult
+                out=spread[:], in0=stats[key]["total"][:], scalar=stats[key]["minus_mean"][:, 0:1],
+                in1=stats[key]["squares"][:, 0:1], op0=ALU.mult, op1=ALU.add,
             )
+            stats[key]["spread"] = spread
+
+        def norm_root(key):
+            scatter = small.tile([P, 1], F32, name="scatter")
+            nc.vector.tensor_scalar(
+                out=scatter[:], in0=stats[key]["spread"][:], scalar1=stats[key]["squares"][:, 1:2], scalar2=0.0,
+                op0=ALU.add, op1=ALU.max,
+            )
+            root = small.tile([P, 1], F32, name="root")
+            nc.gpsimd.tensor_tensor(out=root[:], in0=scatter[:], in1=one_half[:], op=ALU.pow)
+            stats[key]["root"] = root
+
+        def norm_padded(key):
+            padded = small.tile([P, 1], F32, name="padded")
+            nc.vector.tensor_scalar(
+                out=padded[:], in0=stats[key]["root"][:], scalar1=(H - 1) ** -0.5, scalar2=EPS, op0=ALU.mult, op1=ALU.add
+            )
+            stats[key]["padded"] = padded
+
+        def norm_rstd(key):
+            rstd = small.tile([P, 1], F32, name="rstd")
+            nc.vector.reciprocal(out=rstd[:], in_=stats[key]["padded"][:])
+            stats[key]["rstd"] = rstd
+
+        def centre_times_gamma(key, values, gamma_row, half):
             nc.vector.scalar_tensor_tensor(
-                out=values, in0=values, scalar=rstd_of[key][:, 0:1], in1=beta_row[:], op0=ALU.mult, op1=ALU.add
+                out=values[:, columns(half)], in0=values[:, columns(half)], scalar=stats[key]["minus_mean"][:, 0:1],
+                in1=gamma_row[:, columns(half)], op0=ALU.add, op1=ALU.mult,
             )
 
-        def normalise(job):
-            finish_norm(job)
-            if gate_of(job) == GATE_O:
-                scale_and_shift(job, pre[job][:], late_rows["gamma_o"], late_rows["beta_o"])
-            else:
-                nc.vector.tensor_scalar(
-                    out=pre[job][:], in0=pre[job][:], scalar1=mean_of[job][:, 0:1], scalar2=rstd_of[job][:, 0:1],
-                    op0=ALU.subtract, op1=ALU.mult,
-                )
+        def times_rstd_plus_beta(key, values, beta_row, half):
+            nc.vector.scalar_tensor_tensor(
+                out=values[:, columns(half)], in0=values[:, columns(half)], scalar=stats[key]["rstd"][:, 0:1],
+                in1=beta_row[:, columns(half)], op0=ALU.mult, op1=ALU.add,
+            )
 
-        def flip(job):
-            if gate_of(job) == GATE_O:
-                nc.scalar.activation(out=pre[job][:], in_=pre[job][:], func=ACT.Sigmoid)
-                return
-            banks = []
-            for half in range(HALVES):
-                bank = psum.tile([P, BANK_BLOCKS, P], F32, tag="flip", bufs=2)
-                for j in range(BANK_BLOCKS):
-                    block = half * BANK_BLOCKS + j
-                    nc.tensor.transpose(bank[:, j, :], pre[job][:, block * P : (block + 1) * P], ident_f32[:])
-                banks.append(bank)
-            flipped_pre[job] = banks
+        flipped = {}
+        acted = [None] * JOBS
+        state = [None] * B_TILES
+        returned = {}
+        cell = [None] * B_TILES
+        tanh_c = [None] * B_TILES
 
-        def activate(job):
+        def normalise(job, half):
+            nc.vector.tensor_scalar(
+                out=pre[job][:, columns(half)], in0=pre[job][:, columns(half)],
+                scalar1=stats[job]["minus_mean"][:, 0:1], scalar2=stats[job]["rstd"][:, 0:1],
+                op0=ALU.add, op1=ALU.mult,
+            )
+
+        def flip(job, half):
+            bank = flip_bank([P, BANK_BLOCKS, P], F32)
+            for j in range(BANK_BLOCKS):
+                block = half * BANK_BLOCKS + j
+                nc.tensor.transpose(bank[:, j, :], pre[job][:, block * P : (block + 1) * P], ident_f32[:])
+            flipped[(job, half)] = bank
+
+        def activate(job, half):
             gate = gate_of(job)
             bt = job % B_TILES
-            if gate == GATE_O:
-                nc.vector.tensor_tensor(out=tanh_c[bt][:], in0=tanh_c[bt][:], in1=pre[job][:], op=ALU.mult)
-                nc.sync.dma_start(out=out_0[bt * P : (bt + 1) * P, :], in_=tanh_c[bt][:])
-                return
-            if gate == GATE_I:
-                target = jobs.tile([P, UNIT_BLOCKS, P], F32, name="state")
-                state[bt] = target
-            else:
-                target = jobs.tile([P, UNIT_BLOCKS, P], F32, name="flipped_act", bufs=2)
-                flipped_act[job] = target
-            func = ACT.Tanh if gate == GATE_G else ACT.Sigmoid
-            for block in range(UNIT_BLOCKS):
+            if half == 0 and gate == GATE_I:
+                state[bt] = jobs.tile([P, UNIT_BLOCKS, P], F32, name="state")
+            if half == 0 and gate != GATE_I:
+                acted[job] = jobs.tile([P, UNIT_BLOCKS, P], F32, name="acted", bufs=2)
+            target = state[bt] if gate == GATE_I else acted[job]
+            for j in range(BANK_BLOCKS):
+                block = half * BANK_BLOCKS + j
                 column = gate * UNIT_BLOCKS + block
                 nc.scalar.activation(
                     out=target[:, block, :],
-                    in_=flipped_pre[job][block // BANK_BLOCKS][:, block % BANK_BLOCKS, :],
-                    func=func,
+                    in_=flipped[(job, half)][:, j, :],
+                    func=ACT.Tanh if gate == GATE_G else ACT.Sigmoid,
                     scale=norm_cols[:, column : column + 1],
                     bias=norm_cols[:, G * UNIT_BLOCKS + column : G * UNIT_BLOCKS + column + 1],
                 )
 
-        def cell_step(job):
-            gate = gate_of(job)
+        def blocks(half):
+            return slice(half * BANK_BLOCKS, (half + 1) * BANK_BLOCKS)
+
+        def cell_product(job, half):
             bt = job % B_TILES
-            if gate == GATE_G:
-                nc.vector.tensor_tensor(out=state[bt][:], in0=state[bt][:], in1=flipped_act[job][:], op=ALU.mult)
-            if gate == GATE_F:
-                nc.vector.tensor_tensor(out=flipped_act[job][:], in0=flipped_act[job][:], in1=c_t[:, bt], op=ALU.mult)
-                nc.vector.tensor_tensor(out=state[bt][:], in0=state[bt][:], in1=flipped_act[job][:], op=ALU.add)
-
-        def unflip(bt):
-            banks = []
-            for half in range(HALVES):
-                bank = psum.tile([P, BANK_BLOCKS, P], F32, tag="flip", bufs=2)
-                for j in range(BANK_BLOCKS):
-                    nc.tensor.transpose(bank[:, j, :], state[bt][:, half * BANK_BLOCKS + j, :], ident_f32[:])
-                banks.append(bank)
-            cell_banks[bt] = banks
-
-        def cell_sums(bt):
-            cell[bt] = jobs.tile([P, H], F32, name="cell", bufs=2)
-            parts = small.tile([P, HALVES], F32, name="cell_parts")
-            for half in range(HALVES):
-                nc.scalar.activation(
-                    out=cell[bt][:, half * N_TILE : (half + 1) * N_TILE],
-                    in_=cell_banks[bt][half][:].rearrange("p j n -> p (j n)"),
-                    func=ACT.Identity,
-                    accum_out=parts[:, half : half + 1],
+            if gate_of(job) == GATE_G:
+                nc.vector.tensor_tensor(
+                    out=state[bt][:, blocks(half)], in0=state[bt][:, blocks(half)], in1=acted[job][:, blocks(half)], op=ALU.mult
                 )
-            start_norm(("cell", bt), parts[:], cell[bt][:])
+            if gate_of(job) == GATE_F:
+                nc.vector.tensor_tensor(
+                    out=acted[job][:, blocks(half)], in0=acted[job][:, blocks(half)], in1=c_t[:, bt, blocks(half)], op=ALU.mult
+                )
 
-        def cell_norm(bt):
-            finish_norm(("cell", bt))
-            scale_and_shift(("cell", bt), cell[bt][:], late_rows["gamma_c"], late_rows["beta_c"])
-            nc.sync.dma_start(out=out_1[bt * P : (bt + 1) * P, :], in_=cell[bt][:])
+        def cell_sum(job, half):
+            bt = job % B_TILES
+            nc.vector.tensor_tensor(
+                out=state[bt][:, blocks(half)], in0=state[bt][:, blocks(half)], in1=acted[job][:, blocks(half)], op=ALU.add
+            )
 
-        def cell_tanh(bt):
-            tanh_c[bt] = jobs.tile([P, H], F32, name="state")
-            nc.scalar.activation(out=tanh_c[bt][:], in_=cell[bt][:], func=ACT.Tanh)
+        def unflip(name, source, bt, half):
+            bank = flip_bank([P, BANK_BLOCKS, P], F32)
+            for j in range(BANK_BLOCKS):
+                nc.tensor.transpose(bank[:, j, :], source[:, half * BANK_BLOCKS + j, :], ident_f32[:])
+            returned[(name, bt, half)] = bank
 
-        def job_due(k, lag):
-            job, odd = divmod(k - lag, HALVES)
-            return job if odd == 0 and 0 <= job < JOBS else None
+        def cell_out(bt, half):
+            if half == 0:
+                cell[bt] = jobs.tile([P, H], F32, name="cell")
+                stats[("cell", bt)] = {"parts": small.tile([P, HALVES], F32, name="cell_parts")}
+            nc.scalar.activation(
+                out=cell[bt][:, columns(half)],
+                in_=returned[("cell", bt, half)][:].rearrange("p j n -> p (j n)"),
+                func=ACT.Identity,
+                accum_out=stats[("cell", bt)]["parts"][:, half : half + 1],
+            )
 
-        def forget_job_due(k, lag):
-            job = job_due(k, lag)
-            return job if job is not None and gate_of(job) == GATE_F else None
+        def cell_tanh(bt, half):
+            if half == 0:
+                tanh_c[bt] = jobs.tile([P, H], F32, name="state")
+            nc.scalar.activation(out=tanh_c[bt][:, columns(half)], in_=cell[bt][:, columns(half)], func=ACT.Tanh)
+
+        def output(job, half):
+            bt = job % B_TILES
+            nc.vector.tensor_tensor(
+                out=tanh_c[bt][:, columns(half)], in0=returned[("o", bt, half)][:].rearrange("p j n -> p (j n)"),
+                in1=tanh_c[bt][:, columns(half)], op=ALU.mult,
+            )
+            nc.sync.dma_start(out=out_0[bt * P : (bt + 1) * P, columns(half)], in_=tanh_c[bt][:, columns(half)])
+
+        every_gate = GATE_ORDER
+
+        def half_due(k, lag, gates):
+            if not 0 <= k - lag < SLOTS:
+                return None
+            job, half = divmod(k - lag, HALVES)
+            return (job, half) if gate_of(job) in gates else None
+
+        def job_due(k, lag, gates):
+            due = half_due(k, lag, gates)
+            return due[0] if due is not None and due[1] == 0 else None
+
+        def cell_key(job):
+            return ("cell", job % B_TILES)
+
+        def first_small_steps(k):
+            for lag, step in ((LAG_TOTAL, norm_total), (LAG_SPREAD, norm_spread), (LAG_ROOT, norm_root), (LAG_RSTD, norm_padded)):
+                job = job_due(k, lag, every_gate)
+                if job is not None:
+                    step(job)
+            for lag, step in ((LAG_CELL_TOTAL, norm_total), (LAG_CELL_ROOT, norm_spread), (LAG_CELL_RSTD, norm_padded)):
+                job = job_due(k, lag, (GATE_F,))
+                if job is not None:
+                    step(cell_key(job))
+
+        def second_small_steps(k):
+            for lag, step in ((LAG_TOTAL, norm_mean), (LAG_RSTD, norm_rstd)):
+                job = job_due(k, lag, every_gate)
+                if job is not None:
+                    step(job)
+            for lag, step in ((LAG_CELL_TOTAL, norm_mean), (LAG_CELL_ROOT, norm_root), (LAG_CELL_RSTD, norm_rstd)):
+                job = job_due(k, lag, (GATE_F,))
+                if job is not None:
+                    step(cell_key(job))
+
+        prepare_samples(0)
+        for i in range(3):
+            flip_ws(0, i)
+        for first_entry in range(0, len(spread_list), 2):
+            spread_two_rows(first_entry)
+        flip_norm_rows()
 
         slots_a_gate = SLOTS // G
-        for k in range(SLOTS + LAG_CELL_TANH + 1):
+        for k in range(SLOTS + LAST_LAG + 1):
             position, step = divmod(k, slots_a_gate)
             if k < SLOTS:
-                front(k)
-            if k < B_TILES:
-                flip_c(k)
+                job, half = divmod(k, HALVES)
+                matmuls(k)
+                copy_z(k)
+                leave_psum(k, 0, "zb", bias_all[:, gate_of(job), columns(half)], ALU.add)
+            first_small_steps(k)
+            if k < SLOTS:
+                leave_psum(k, 1, "xh", terms["zx"][:], ALU.mult)
+            second_small_steps(k)
+            if k < SLOTS:
+                leave_psum(k, 2, "hh", terms["zh"][:], ALU.mult)
+                add_terms(k)
+
+            due = half_due(k, LAG_ACTIVATE, every_gate)
+            if due is not None:
+                activate(due[0], due[1])
+            due = half_due(k, LAG_SQUARE, every_gate)
+            if due is not None:
+                square_half(due[0], pre[due[0]], due[1])
+            due = half_due(k, LAG_CELL_OUT, (GATE_F,))
+            if due is not None:
+                cell_out(due[0] % B_TILES, due[1])
+            due = half_due(k, LAG_CELL_SQUARE, (GATE_F,))
+            if due is not None:
+                square_half(cell_key(due[0]), cell[due[0] % B_TILES], due[1])
+            due = half_due(k, LAG_CELL_TANH, (GATE_F,))
+            if due is not None:
+                cell_tanh(due[0] % B_TILES, due[1])
+
+            due = half_due(k, LAG_CELL, (GATE_G, GATE_F))
+            if due is not None:
+                cell_product(due[0], due[1])
+            due = half_due(k, LAG_NORMALISE, every_gate)
+            if due is not None:
+                normalise(due[0], due[1])
+            due = half_due(k, LAG_CELL, (GATE_F,))
+            if due is not None:
+                cell_sum(due[0], due[1])
+            due = half_due(k, LAG_CELL_NORMALISE, (GATE_F,))
+            if due is not None:
+                centre_times_gamma(cell_key(due[0]), cell[due[0] % B_TILES], gamma_c, due[1])
+            due = half_due(k, LAG_OUTPUT, (GATE_O,))
+            if due is not None:
+                output(due[0], due[1])
+            due = half_due(k, LAG_CELL_SHIFT, (GATE_F,))
+            if due is not None:
+                bt = due[0] % B_TILES
+                times_rstd_plus_beta(cell_key(due[0]), cell[bt], beta_c, due[1])
+                nc.sync.dma_start(out=out_1[bt * P : (bt + 1) * P, columns(due[1])], in_=cell[bt][:, columns(due[1])])
+
+            due = half_due(k, LAG_FLIP, every_gate)
+            if due is not None:
+                flip(due[0], due[1])
+            due = half_due(k, LAG_UNFLIP, (GATE_F,))
+            if due is not None:
+                unflip("cell", state[due[0] % B_TILES], due[0] % B_TILES, due[1])
+            due = half_due(k, LAG_RETURN, (GATE_O,))
+            if due is not None:
+                unflip("o", acted[due[0]], due[0] % B_TILES, due[1])
+
+            if k % 2 == 0 and k // 2 + 1 < B_TILES:
+                prepare_samples(k // 2 + 1)
+            if position == 1 and step < B_TILES:
+                flip_c(step)
             if step == 1 and 1 <= position < G - 1:
-                load_gate(position + 1)
-            if k == slots_a_gate + 1:
-                load_late_rows()
+                load_ws(position + 1)
+                load_words(position + 1)
             if 4 <= step < 7 and position < G - 1:
                 flip_ws(position + 1, step - 4)
-            job = forget_job_due(k, LAG_CELL_TANH)
-            if job is not None:
-                cell_tanh(job % B_TILES)
-            job = forget_job_due(k, LAG_CELL_NORM)
-            if job is not None:
-                cell_norm(job % B_TILES)
-            job = forget_job_due(k, LAG_CELL_SUMS)
-            if job is not None:
-                cell_sums(job % B_TILES)
-            job = job_due(k, LAG_CELL)
-            if job is not None:
-                cell_step(job)
-            job = job_due(k, LAG_ACTIVATE)
-            if job is not None:
-                activate(job)
-            job = forget_job_due(k, LAG_UNFLIP)
-            if job is not None:
-                unflip(job % B_TILES)
-            job = job_due(k, LAG_FLIP)
-            if job is not None:
-                flip(job)
-            job = job_due(k, LAG_NORMALISE)
-            if job is not None:
-                normalise(job)
-            job = job_due(k, LAG_SUMS)
-            if job is not None:
-                start_norm(job, sum_parts[job][:], pre[job][:])

@@ -135,23 +135,22 @@ def tile_hyperlstmcell_pb_kernel(
                 raws.append(raw)
             ws_raw[position] = raws
 
-        def load_words(position):
+        def load_words(position, half):
             gate = GATE_ORDER[position]
-            words = per_gate.tile([P, 2, PASSES, H], U32, name="w_words", align_bytes=64)
+            if half == 0:
+                w_words[position] = per_gate.tile([P, 2, PASSES, H], U32, name="w_words", align_bytes=64)
+            first_unit = gate * H + half * N_TILE
             for operand, source in enumerate((Wih_words, Whh_words)):
                 for g in range(PASSES):
                     nc.sync.dma_start(
-                        out=words[:, operand, g, :].bitcast(I32),
-                        in_=source[g, :, gate * H : (gate + 1) * H, :].rearrange("p n t -> p (n t)").bitcast(I32),
+                        out=w_words[position][:, operand, g, half * N_TILE : (half + 1) * N_TILE].bitcast(I32),
+                        in_=source[g, :, first_unit : first_unit + N_TILE, :].rearrange("p n t -> p (n t)").bitcast(I32),
                     )
-            w_words[position] = words
 
-        row_sources = (bias, lnc_gamma, lnc_beta)
-        first = 0
-        for source in row_sources:
-            count = source.shape[0] // N_TILE
-            nc.gpsimd.dma_start(out=rows[first : first + count, :], in_=source.rearrange("(r n) -> r n", n=N_TILE))
-            first += count
+        nc.gpsimd.dma_start(
+            out=rows[0:HALVES, :],
+            in_=bias[GATE_ORDER[0] * H : (GATE_ORDER[0] + 1) * H].rearrange("(r n) -> r n", n=N_TILE),
+        )
         for i, source in enumerate((ln_gamma, ln_beta)):
             nc.gpsimd.dma_start(
                 out=norm_rows[i * G * UNIT_BLOCKS : (i + 1) * G * UNIT_BLOCKS, :],
@@ -160,6 +159,7 @@ def tile_hyperlstmcell_pb_kernel(
 
         load_samples(0)
         load_ws(0)
+        load_words(0, 0)
         for operand, source in enumerate((Wih_scales, Whh_scales)):
             for quad in range(4):
                 first = 32 * quad + 8 * operand
@@ -167,19 +167,27 @@ def tile_hyperlstmcell_pb_kernel(
                     out=planes[first : first + 8, :].bitcast(I32),
                     in_=source[:, 4 * quad : 4 * quad + 4, :].bitcast(I32),
                 )
-        load_words(0)
+        load_words(0, 1)
         for bt in range(1, B_TILES):
             load_samples(bt)
         load_ws(1)
-        load_words(1)
+        for half in range(HALVES):
+            load_words(1, half)
         c_raw = const.tile([P, B_TILES, H], BF16)
         nc.sync.dma_start(out=c_raw[:], in_=c.rearrange("(t p) n -> p t n", p=P))
+        bias_all = const.tile([P, G, H], BF16)
+        for gate in GATE_ORDER[1:]:
+            nc.sync.dma_start(out=bias_all[:, gate, :], in_=bias[gate * H : (gate + 1) * H].partition_broadcast(P))
+        gamma_c = const.tile([P, H], BF16)
+        nc.sync.dma_start(out=gamma_c[:], in_=lnc_gamma.partition_broadcast(P))
+        beta_c = const.tile([P, H], BF16)
+        nc.sync.dma_start(out=beta_c[:], in_=lnc_beta.partition_broadcast(P))
 
         act_codes = const.tile([P, 2, B_TILES, PASSES, P], U32, align_bytes=64)
         act_scales = const.tile([P, 2, B_TILES, PASSES, P], U8, align_bytes=64)
         emb_t = [const.tile([P, G, B], BF16, name="emb_t%d" % i) for i in range(3)]
 
-        def prepare_samples(bt):
+        def prepare_activations(bt):
             grouped = []
             for operand in range(2):
                 words = act_raw[bt][:, operand, :].bitcast(F32)
@@ -201,6 +209,8 @@ def tile_hyperlstmcell_pb_kernel(
                     scales=act_scales[:, operand, bt].rearrange("p g b -> p (g b)"),
                     in_=grouped[operand][:],
                 )
+
+        def prepare_embeddings(bt):
             for i in range(3):
                 emb_flip = flip_bank([P, G, P], BF16)
                 for gate in range(G):
@@ -223,26 +233,13 @@ def tile_hyperlstmcell_pb_kernel(
                 nc.tensor.transpose(c_flip[:, j, :], c_raw[:, bt, j * P : (j + 1) * P], ident_bf[:])
             nc.scalar.copy(out=c_t[:, bt], in_=c_flip[:])
 
-        bias_all = const.tile([P, G, H], BF16)
-        gamma_c = const.tile([P, H], BF16)
-        beta_c = const.tile([P, H], BF16)
-        spread_list = []
-        for gate in GATE_ORDER:
-            for half in range(HALVES):
-                spread_list.append((gate * HALVES + half, bias_all[:, gate, half * N_TILE : (half + 1) * N_TILE]))
-        for i, target in enumerate((gamma_c, beta_c)):
-            for half in range(HALVES):
-                spread_list.append(((G + i) * HALVES + half, target[:, half * N_TILE : (half + 1) * N_TILE]))
-
-        def spread_two_rows(first_entry):
-            copies = (nc.scalar.copy, nc.vector.tensor_copy)
-            for entry in range(2):
-                r, target = spread_list[first_entry + entry]
+        def spread_first_bias():
+            for r, copy_out in enumerate((nc.scalar.copy, nc.vector.tensor_copy)):
                 repeated = flip_bank([P, N_TILE], F32)
                 nc.tensor.matmul(
                     out=repeated[:], lhsT=ident_bf[:, r : r + 1].to_broadcast([P, P]), rhs=rows[:], start=True, stop=True
                 )
-                copies[entry](out=target, in_=repeated[:])
+                copy_out(out=bias_all[:, GATE_ORDER[0], r * N_TILE : (r + 1) * N_TILE], in_=repeated[:])
 
         norm_cols = const.tile([P, 2 * G * UNIT_BLOCKS], F32)
 
@@ -290,7 +287,7 @@ def tile_hyperlstmcell_pb_kernel(
                 banks[tag] = acc
             if half == 0:
                 pre[job] = jobs.tile([P, H], F32, name="pre")
-                stats[job] = {"parts": small.tile([P, 3 * HALVES], F32, name="parts")}
+                stats[job] = {"parts": small.tile([P, 2 * HALVES], F32, name="parts")}
 
         def copy_z(k):
             for tag in ("zx", "zh"):
@@ -298,20 +295,24 @@ def tile_hyperlstmcell_pb_kernel(
                 nc.scalar.copy(out=z_sb[:], in_=banks[tag][:])
                 terms[tag] = z_sb
 
-        def leave_psum(k, part, tag, other, op):
-            job, half = divmod(k, HALVES)
-            column = 3 * half + part
+        def leave_psum(tag, other, op):
             term = work.tile([P, N_TILE], F32, name="term_" + tag)
-            nc.vector.scalar_tensor_tensor(
-                out=term[:], in0=banks[tag][:], scalar=1.0, in1=other, op0=ALU.mult, op1=op,
-                accum_out=stats[job]["parts"][:, column : column + 1],
-            )
+            nc.vector.tensor_tensor(out=term[:], in0=banks[tag][:], in1=other, op=op)
             terms[tag] = term
 
-        def add_terms(k):
+        def last_term_and_sums(k):
             job, half = divmod(k, HALVES)
-            nc.gpsimd.tensor_tensor(out=terms["xh"][:], in0=terms["xh"][:], in1=terms["hh"][:], op=ALU.add)
-            nc.gpsimd.tensor_tensor(out=pre[job][:, columns(half)], in0=terms["xh"][:], in1=terms["zb"][:], op=ALU.add)
+            parts = stats[job]["parts"]
+            term = work.tile([P, N_TILE], F32, name="term_hh")
+            nc.vector.scalar_tensor_tensor(
+                out=term[:], in0=banks["hh"][:], scalar=1.0, in1=terms["zh"][:], op0=ALU.mult, op1=ALU.mult,
+                accum_out=parts[:, 2 * half : 2 * half + 1],
+            )
+            nc.vector.scalar_tensor_tensor(
+                out=terms["xh"][:], in0=terms["xh"][:], scalar=1.0, in1=terms["zb"][:], op0=ALU.mult, op1=ALU.add,
+                accum_out=parts[:, 2 * half + 1 : 2 * half + 2],
+            )
+            nc.gpsimd.tensor_tensor(out=pre[job][:, columns(half)], in0=terms["xh"][:], in1=term[:], op=ALU.add)
 
         def square_half(key, values, half):
             if half == 0:
@@ -501,11 +502,11 @@ def tile_hyperlstmcell_pb_kernel(
                 if job is not None:
                     step(cell_key(job))
 
-        prepare_samples(0)
+        prepare_activations(0)
+        prepare_embeddings(0)
         for i in range(3):
             flip_ws(0, i)
-        for first_entry in range(0, len(spread_list), 2):
-            spread_two_rows(first_entry)
+        spread_first_bias()
         flip_norm_rows()
 
         slots_a_gate = SLOTS // G
@@ -515,14 +516,13 @@ def tile_hyperlstmcell_pb_kernel(
                 job, half = divmod(k, HALVES)
                 matmuls(k)
                 copy_z(k)
-                leave_psum(k, 0, "zb", bias_all[:, gate_of(job), columns(half)], ALU.add)
+                leave_psum("zb", bias_all[:, gate_of(job), columns(half)], ALU.add)
             first_small_steps(k)
             if k < SLOTS:
-                leave_psum(k, 1, "xh", terms["zx"][:], ALU.mult)
+                leave_psum("xh", terms["zx"][:], ALU.mult)
             second_small_steps(k)
             if k < SLOTS:
-                leave_psum(k, 2, "hh", terms["zh"][:], ALU.mult)
-                add_terms(k)
+                last_term_and_sums(k)
 
             due = half_due(k, LAG_ACTIVATE, every_gate)
             if due is not None:
@@ -571,12 +571,16 @@ def tile_hyperlstmcell_pb_kernel(
             if due is not None:
                 unflip("o", acted[due[0]], due[0] % B_TILES, due[1])
 
-            if k % 2 == 0 and k // 2 + 1 < B_TILES:
-                prepare_samples(k // 2 + 1)
+            if k // 2 + 1 < B_TILES:
+                if k % 2 == 0:
+                    prepare_activations(k // 2 + 1)
+                else:
+                    prepare_embeddings(k // 2 + 1)
             if position == 1 and step < B_TILES:
                 flip_c(step)
             if step == 1 and 1 <= position < G - 1:
                 load_ws(position + 1)
-                load_words(position + 1)
+                for half in range(HALVES):
+                    load_words(position + 1, half)
             if 4 <= step < 7 and position < G - 1:
                 flip_ws(position + 1, step - 4)

@@ -147,10 +147,7 @@ def tile_hyperlstmcell_pb_kernel(
                         in_=source[g, :, first_unit : first_unit + N_TILE, :].rearrange("p n t -> p (n t)").bitcast(I32),
                     )
 
-        nc.gpsimd.dma_start(
-            out=rows[0:HALVES, :],
-            in_=bias[GATE_ORDER[0] * H : (GATE_ORDER[0] + 1) * H].rearrange("(r n) -> r n", n=N_TILE),
-        )
+        nc.gpsimd.dma_start(out=rows[0 : G * HALVES, :], in_=bias.rearrange("(r n) -> r n", n=N_TILE))
         for i, source in enumerate((ln_gamma, ln_beta)):
             nc.gpsimd.dma_start(
                 out=norm_rows[i * G * UNIT_BLOCKS : (i + 1) * G * UNIT_BLOCKS, :],
@@ -175,9 +172,6 @@ def tile_hyperlstmcell_pb_kernel(
             load_words(1, half)
         c_raw = const.tile([P, B_TILES, H], BF16)
         nc.sync.dma_start(out=c_raw[:], in_=c.rearrange("(t p) n -> p t n", p=P))
-        bias_all = const.tile([P, G, H], BF16)
-        for gate in GATE_ORDER[1:]:
-            nc.sync.dma_start(out=bias_all[:, gate, :], in_=bias[gate * H : (gate + 1) * H].partition_broadcast(P))
         gamma_c = const.tile([P, H], BF16)
         nc.sync.dma_start(out=gamma_c[:], in_=lnc_gamma.partition_broadcast(P))
         beta_c = const.tile([P, H], BF16)
@@ -233,13 +227,17 @@ def tile_hyperlstmcell_pb_kernel(
                 nc.tensor.transpose(c_flip[:, j, :], c_raw[:, bt, j * P : (j + 1) * P], ident_bf[:])
             nc.scalar.copy(out=c_t[:, bt], in_=c_flip[:])
 
+        first_bias = const.tile([P, H], BF16)
+
+        def row_picker(gate, half):
+            r = gate * HALVES + half
+            return ident_bf[:, r : r + 1].to_broadcast([P, P])
+
         def spread_first_bias():
-            for r, copy_out in enumerate((nc.scalar.copy, nc.vector.tensor_copy)):
+            for half, copy_out in enumerate((nc.scalar.copy, nc.vector.tensor_copy)):
                 repeated = flip_bank([P, N_TILE], F32)
-                nc.tensor.matmul(
-                    out=repeated[:], lhsT=ident_bf[:, r : r + 1].to_broadcast([P, P]), rhs=rows[:], start=True, stop=True
-                )
-                copy_out(out=bias_all[:, GATE_ORDER[0], r * N_TILE : (r + 1) * N_TILE], in_=repeated[:])
+                nc.tensor.matmul(out=repeated[:], lhsT=row_picker(GATE_ORDER[0], half), rhs=rows[:], start=True, stop=True)
+                copy_out(out=first_bias[:, half * N_TILE : (half + 1) * N_TILE], in_=repeated[:])
 
         norm_cols = const.tile([P, 2 * G * UNIT_BLOCKS], F32)
 
@@ -264,13 +262,19 @@ def tile_hyperlstmcell_pb_kernel(
             position, bt = divmod(job, B_TILES)
             gate = GATE_ORDER[position]
             samples = slice(bt * P, (bt + 1) * P)
-            for i, tag in ((2, "zb"), (0, "zx"), (1, "zh")):
-                z = psum.tile([P, N_TILE], F32, name=tag)
-                nc.tensor.matmul(
-                    out=z[:], lhsT=emb_t[i][:, gate, samples], rhs=ws_t[position][i][:, columns(half)],
-                    start=True, stop=True,
-                )
-                banks[tag] = z
+            def plain_matmuls(plain):
+                for i, tag in plain:
+                    z = psum.tile([P, N_TILE], F32, name=tag)
+                    with_bias = tag == "zb" and position > 0
+                    nc.tensor.matmul(
+                        out=z[:], lhsT=emb_t[i][:, gate, samples], rhs=ws_t[position][i][:, columns(half)],
+                        start=True, stop=not with_bias,
+                    )
+                    if with_bias:
+                        nc.tensor.matmul(out=z[:], lhsT=row_picker(gate, half), rhs=rows[:], start=False, stop=True)
+                    banks[tag] = z
+
+            plain_matmuls(((0, "zx"), (1, "zh")))
             for operand, tag in enumerate(("xh", "hh")):
                 acc = psum.tile([P, N_TILE], F32, name=tag)
                 for g in range(PASSES):
@@ -285,6 +289,7 @@ def tile_hyperlstmcell_pb_kernel(
                         stop=(g == PASSES - 1),
                     )
                 banks[tag] = acc
+            plain_matmuls(((2, "zb"),))
             if half == 0:
                 pre[job] = jobs.tile([P, H], F32, name="pre")
                 stats[job] = {"parts": small.tile([P, 2 * HALVES], F32, name="parts")}
@@ -300,19 +305,25 @@ def tile_hyperlstmcell_pb_kernel(
             nc.vector.tensor_tensor(out=term[:], in0=banks[tag][:], in1=other, op=op)
             terms[tag] = term
 
-        def last_term_and_sums(k):
+        def product_h(k):
             job, half = divmod(k, HALVES)
             parts = stats[job]["parts"]
             term = work.tile([P, N_TILE], F32, name="term_hh")
+            terms["hh"] = term
             nc.vector.scalar_tensor_tensor(
                 out=term[:], in0=banks["hh"][:], scalar=1.0, in1=terms["zh"][:], op0=ALU.mult, op1=ALU.mult,
                 accum_out=parts[:, 2 * half : 2 * half + 1],
             )
+
+        def sum_terms(k):
+            job, half = divmod(k, HALVES)
+            parts = stats[job]["parts"]
+            shift = terms["zb"] if job < B_TILES else banks["zb"]
             nc.vector.scalar_tensor_tensor(
-                out=terms["xh"][:], in0=terms["xh"][:], scalar=1.0, in1=terms["zb"][:], op0=ALU.mult, op1=ALU.add,
+                out=terms["xh"][:], in0=shift[:], scalar=1.0, in1=terms["xh"][:], op0=ALU.mult, op1=ALU.add,
                 accum_out=parts[:, 2 * half + 1 : 2 * half + 2],
             )
-            nc.gpsimd.tensor_tensor(out=pre[job][:, columns(half)], in0=terms["xh"][:], in1=term[:], op=ALU.add)
+            nc.gpsimd.tensor_tensor(out=pre[job][:, columns(half)], in0=terms["xh"][:], in1=terms["hh"][:], op=ALU.add)
 
         def square_half(key, values, half):
             if half == 0:
@@ -516,13 +527,15 @@ def tile_hyperlstmcell_pb_kernel(
                 job, half = divmod(k, HALVES)
                 matmuls(k)
                 copy_z(k)
-                leave_psum("zb", bias_all[:, gate_of(job), columns(half)], ALU.add)
+                leave_psum("xh", terms["zx"][:], ALU.mult)
             first_small_steps(k)
             if k < SLOTS:
-                leave_psum("xh", terms["zx"][:], ALU.mult)
+                if position == 0:
+                    leave_psum("zb", first_bias[:, columns(half)], ALU.add)
+                product_h(k)
             second_small_steps(k)
             if k < SLOTS:
-                last_term_and_sums(k)
+                sum_terms(k)
 
             due = half_due(k, LAG_ACTIVATE, every_gate)
             if due is not None:

@@ -154,19 +154,24 @@ def tile_hyperlstmcell_pb_kernel(
                 in_=source.rearrange("g (j p) -> (g j) p", p=P),
             )
 
+        def load_scales(first_gate, gates):
+            scale_columns = slice(first_gate * H, (first_gate + gates) * H)
+            for operand, source in enumerate((Wih_scales, Whh_scales)):
+                for quad in range(4):
+                    first = 32 * quad + 8 * operand
+                    nc.sync.dma_start(
+                        out=planes[first : first + 8, scale_columns].bitcast(I32),
+                        in_=source[:, 4 * quad : 4 * quad + 4, scale_columns].bitcast(I32),
+                    )
+
         load_samples(0)
         load_ws(0)
         load_words(0, 0)
-        for operand, source in enumerate((Wih_scales, Whh_scales)):
-            for quad in range(4):
-                first = 32 * quad + 8 * operand
-                nc.sync.dma_start(
-                    out=planes[first : first + 8, :].bitcast(I32),
-                    in_=source[:, 4 * quad : 4 * quad + 4, :].bitcast(I32),
-                )
+        load_scales(GATE_ORDER[0], 1)
         load_words(0, 1)
         for bt in range(1, B_TILES):
             load_samples(bt)
+        load_scales(1, G - 1)
         load_ws(1)
         for half in range(HALVES):
             load_words(1, half)

@@ -113,11 +113,13 @@ def tile_hyperlstmcell_pb_kernel(
         act_raw = [None] * B_TILES
         emb_raw = [None] * B_TILES
 
-        def load_samples(bt):
+        def load_activations(bt):
             act_raw[bt] = jobs.tile([P, 2, K], BF16, name="cell")
-            emb_raw[bt] = jobs.tile([P, 3, G * E], BF16, name="state")
             for operand, source in enumerate((x, h)):
                 nc.sync.dma_start(out=act_raw[bt][:, operand, :], in_=source[bt * P : (bt + 1) * P, :])
+
+        def load_embeddings(bt):
+            emb_raw[bt] = jobs.tile([P, 3, G * E], BF16, name="state")
             for i, source in enumerate((emb_x, emb_h, emb_b)):
                 nc.sync.dma_start(
                     out=emb_raw[bt][:, i, :], in_=source[bt * P : (bt + 1) * P].rearrange("p g e -> p (g e)")
@@ -154,24 +156,28 @@ def tile_hyperlstmcell_pb_kernel(
                 in_=source.rearrange("g (j p) -> (g j) p", p=P),
             )
 
-        def load_scales(first_gate, gates):
-            scale_columns = slice(first_gate * H, (first_gate + gates) * H)
+        def load_scales(first_column, last_column):
             for operand, source in enumerate((Wih_scales, Whh_scales)):
                 for quad in range(4):
                     first = 32 * quad + 8 * operand
                     nc.sync.dma_start(
-                        out=planes[first : first + 8, scale_columns].bitcast(I32),
-                        in_=source[:, 4 * quad : 4 * quad + 4, scale_columns].bitcast(I32),
+                        out=planes[first : first + 8, first_column:last_column].bitcast(I32),
+                        in_=source[:, 4 * quad : 4 * quad + 4, first_column:last_column].bitcast(I32),
                     )
 
-        load_samples(0)
+        load_activations(0)
+        load_embeddings(0)
         load_ws(0)
         load_words(0, 0)
-        load_scales(GATE_ORDER[0], 1)
+        load_scales(0, N_TILE)
+        load_activations(1)
+        load_scales(N_TILE, H)
         load_words(0, 1)
-        for bt in range(1, B_TILES):
-            load_samples(bt)
-        load_scales(1, G - 1)
+        load_embeddings(1)
+        for bt in range(2, B_TILES):
+            load_activations(bt)
+            load_embeddings(bt)
+        load_scales(H, G * H)
         load_ws(1)
         for half in range(HALVES):
             load_words(1, half)

@@ -34,9 +34,8 @@ GATE_ORDER = (GATE_I, GATE_G, GATE_F, GATE_O)
 JOBS = G * B_TILES
 SLOTS = JOBS * HALVES
 
-LAG_SQUARE = 2
-LAG_TOTAL = 2
-LAG_SPREAD = 3
+LAG_MEAN = 2
+LAG_SQUARE = 3
 LAG_ROOT = 4
 LAG_RSTD = 5
 LAG_NORMALISE = 5
@@ -47,11 +46,11 @@ LAG_RETURN = 8
 LAG_OUTPUT = 9
 LAG_UNFLIP = 9
 LAG_CELL_OUT = 10
-LAG_CELL_SQUARE = 11
-LAG_CELL_TOTAL = 12
-LAG_CELL_ROOT = 13
-LAG_CELL_RSTD = 14
+LAG_CELL_MEAN = 12
+LAG_CELL_SQUARE = 13
+LAG_CELL_ROOT = 14
 LAG_CELL_NORMALISE = 14
+LAG_CELL_RSTD = 15
 LAG_CELL_SHIFT = 15
 LAG_CELL_TANH = 16
 LAST_LAG = LAG_CELL_TANH + 1
@@ -227,7 +226,8 @@ def tile_hyperlstmcell_pb_kernel(
             for j in range(UNIT_BLOCKS):
                 nc.tensor.transpose(ws_flip[:, j, :], ws_raw[position][i][:, j, :], ident_bf[:])
             flat = per_gate.tile([P, H], BF16, name="ws_t%d" % i)
-            nc.scalar.copy(out=flat[:], in_=ws_flip[:].rearrange("p j n -> p (j n)"))
+            copy_out = nc.scalar.copy if position == 0 else nc.vector.tensor_copy
+            copy_out(out=flat[:], in_=ws_flip[:].rearrange("p j n -> p (j n)"))
             ws_t[position][i] = flat
 
         c_t = const.tile([P, B_TILES, UNIT_BLOCKS, P], BF16)
@@ -236,7 +236,7 @@ def tile_hyperlstmcell_pb_kernel(
             c_flip = flip_bank([P, UNIT_BLOCKS, P], BF16)
             for j in range(UNIT_BLOCKS):
                 nc.tensor.transpose(c_flip[:, j, :], c_raw[:, bt, j * P : (j + 1) * P], ident_bf[:])
-            nc.scalar.copy(out=c_t[:, bt], in_=c_flip[:])
+            nc.vector.tensor_copy(out=c_t[:, bt], in_=c_flip[:])
 
         first_bias = const.tile([P, H], BF16)
 
@@ -336,49 +336,30 @@ def tile_hyperlstmcell_pb_kernel(
             )
             nc.gpsimd.tensor_tensor(out=pre[job][:, columns(half)], in0=terms["xh"][:], in1=terms["hh"][:], op=ALU.add)
 
-        def square_half(key, values, half):
-            if half == 0:
-                stats[key]["squares"] = small.tile([P, HALVES], F32, name="squares")
-            scratch = work.tile([P, N_TILE], BF16, name="scratch", bufs=2)
-            nc.scalar.activation(
-                out=scratch[:], in_=values[:, columns(half)], func=ACT.Square,
-                accum_out=stats[key]["squares"][:, half : half + 1],
-            )
-
-        def norm_total(key):
-            total = small.tile([P, 1], F32, name="total")
-            nc.vector.tensor_reduce(out=total[:], in_=stats[key]["parts"][:], axis=AXIS.X, op=ALU.add)
-            stats[key]["total"] = total
-
         def norm_mean(key):
+            parts = stats[key]["parts"]
             minus_mean = small.tile([P, 1], F32, name="minus_mean")
+            scaled = small.tile([P, 2 * HALVES], F32, name="scaled")
             nc.vector.tensor_scalar(
-                out=minus_mean[:], in0=stats[key]["total"][:], scalar1=-1.0 / H, scalar2=None, op0=ALU.mult
+                out=scaled[:, 0 : parts.shape[1]], in0=parts[:], scalar1=-1.0 / H, scalar2=None, op0=ALU.mult, op1=ALU.add,
+                accum_out=minus_mean[:],
             )
             stats[key]["minus_mean"] = minus_mean
 
-        def norm_spread(key):
-            spread = small.tile([P, 1], F32, name="spread")
-            nc.vector.scalar_tensor_tensor(
-                out=spread[:], in0=stats[key]["total"][:], scalar=stats[key]["minus_mean"][:, 0:1],
-                in1=stats[key]["squares"][:, 0:1], op0=ALU.mult, op1=ALU.add,
+        def square_job(key, values):
+            scatter = small.tile([P, 1], F32, name="scatter")
+            scratch = work.tile([P, H], BF16, name="scratch", bufs=2)
+            nc.scalar.activation(
+                out=scratch[:], in_=values[:], func=ACT.Square, bias=stats[key]["minus_mean"][:, 0:1], accum_out=scatter[:]
             )
-            stats[key]["spread"] = spread
+            stats[key]["scatter"] = scatter
 
         def norm_root(key):
-            scatter = small.tile([P, 1], F32, name="scatter")
-            nc.vector.tensor_scalar(
-                out=scatter[:], in0=stats[key]["spread"][:], scalar1=stats[key]["squares"][:, 1:2], scalar2=0.0,
-                op0=ALU.add, op1=ALU.max,
-            )
             root = small.tile([P, 1], F32, name="root")
-            nc.gpsimd.tensor_tensor(out=root[:], in0=scatter[:], in1=one_half[:], op=ALU.pow)
-            stats[key]["root"] = root
-
-        def norm_padded(key):
+            nc.gpsimd.tensor_tensor(out=root[:], in0=stats[key]["scatter"][:], in1=one_half[:], op=ALU.pow)
             padded = small.tile([P, 1], F32, name="padded")
-            nc.vector.tensor_scalar(
-                out=padded[:], in0=stats[key]["root"][:], scalar1=(H - 1) ** -0.5, scalar2=EPS, op0=ALU.mult, op1=ALU.add
+            nc.gpsimd.tensor_scalar(
+                out=padded[:], in0=root[:], scalar1=(H - 1) ** -0.5, scalar2=EPS, op0=ALU.mult, op1=ALU.add
             )
             stats[key]["padded"] = padded
 
@@ -504,25 +485,13 @@ def tile_hyperlstmcell_pb_kernel(
         def cell_key(job):
             return ("cell", job % B_TILES)
 
-        def first_small_steps(k):
-            for lag, step in ((LAG_TOTAL, norm_total), (LAG_SPREAD, norm_spread), (LAG_ROOT, norm_root), (LAG_RSTD, norm_padded)):
-                job = job_due(k, lag, every_gate)
-                if job is not None:
-                    step(job)
-            for lag, step in ((LAG_CELL_TOTAL, norm_total), (LAG_CELL_ROOT, norm_spread), (LAG_CELL_RSTD, norm_padded)):
-                job = job_due(k, lag, (GATE_F,))
-                if job is not None:
-                    step(cell_key(job))
-
-        def second_small_steps(k):
-            for lag, step in ((LAG_TOTAL, norm_mean), (LAG_RSTD, norm_rstd)):
-                job = job_due(k, lag, every_gate)
-                if job is not None:
-                    step(job)
-            for lag, step in ((LAG_CELL_TOTAL, norm_mean), (LAG_CELL_ROOT, norm_root), (LAG_CELL_RSTD, norm_rstd)):
-                job = job_due(k, lag, (GATE_F,))
-                if job is not None:
-                    step(cell_key(job))
+        def small_step(k, gate_lag, cell_lag, step):
+            job = job_due(k, gate_lag, every_gate)
+            if job is not None:
+                step(job)
+            job = job_due(k, cell_lag, (GATE_F,))
+            if job is not None:
+                step(cell_key(job))
 
         prepare_activations(0)
         prepare_embeddings(0)
@@ -539,27 +508,28 @@ def tile_hyperlstmcell_pb_kernel(
                 matmuls(k)
                 copy_z(k)
                 leave_psum("xh", terms["zx"][:], ALU.mult)
-            first_small_steps(k)
+            small_step(k, LAG_MEAN, LAG_CELL_MEAN, norm_mean)
+            small_step(k, LAG_ROOT, LAG_CELL_ROOT, norm_root)
             if k < SLOTS:
                 if position == 0:
                     leave_psum("zb", first_bias[:, columns(half)], ALU.add)
                 product_h(k)
-            second_small_steps(k)
+            small_step(k, LAG_RSTD, LAG_CELL_RSTD, norm_rstd)
             if k < SLOTS:
                 sum_terms(k)
 
             due = half_due(k, LAG_ACTIVATE, every_gate)
             if due is not None:
                 activate(due[0], due[1])
-            due = half_due(k, LAG_SQUARE, every_gate)
-            if due is not None:
-                square_half(due[0], pre[due[0]], due[1])
+            job_to_square = job_due(k, LAG_SQUARE, every_gate)
+            if job_to_square is not None:
+                square_job(job_to_square, pre[job_to_square])
             due = half_due(k, LAG_CELL_OUT, (GATE_F,))
             if due is not None:
                 cell_out(due[0] % B_TILES, due[1])
-            due = half_due(k, LAG_CELL_SQUARE, (GATE_F,))
-            if due is not None:
-                square_half(cell_key(due[0]), cell[due[0] % B_TILES], due[1])
+            job_to_square = job_due(k, LAG_CELL_SQUARE, (GATE_F,))
+            if job_to_square is not None:
+                square_job(cell_key(job_to_square), cell[job_to_square % B_TILES])
             due = half_due(k, LAG_CELL_TANH, (GATE_F,))
             if due is not None:
                 cell_tanh(due[0] % B_TILES, due[1])

@@ -226,8 +226,7 @@ def tile_hyperlstmcell_pb_kernel(
             for j in range(UNIT_BLOCKS):
                 nc.tensor.transpose(ws_flip[:, j, :], ws_raw[position][i][:, j, :], ident_bf[:])
             flat = per_gate.tile([P, H], BF16, name="ws_t%d" % i)
-            copy_out = nc.scalar.copy if position == 0 else nc.vector.tensor_copy
-            copy_out(out=flat[:], in_=ws_flip[:].rearrange("p j n -> p (j n)"))
+            nc.scalar.copy(out=flat[:], in_=ws_flip[:].rearrange("p j n -> p (j n)"))
             ws_t[position][i] = flat
 
         c_t = const.tile([P, B_TILES, UNIT_BLOCKS, P], BF16)
@@ -236,7 +235,7 @@ def tile_hyperlstmcell_pb_kernel(
             c_flip = flip_bank([P, UNIT_BLOCKS, P], BF16)
             for j in range(UNIT_BLOCKS):
                 nc.tensor.transpose(c_flip[:, j, :], c_raw[:, bt, j * P : (j + 1) * P], ident_bf[:])
-            nc.vector.tensor_copy(out=c_t[:, bt], in_=c_flip[:])
+            nc.scalar.copy(out=c_t[:, bt], in_=c_flip[:])
 
         first_bias = const.tile([P, H], BF16)
 

@@ -164,20 +164,26 @@ def tile_hyperlstmcell_pb_kernel(
                         in_=source[:, 4 * quad : 4 * quad + 4, first_column:last_column].bitcast(I32),
                     )
 
+        def load_gate_scales(position):
+            first_column = GATE_ORDER[position] * H
+            load_scales(first_column, first_column + H)
+
+        first_column = GATE_ORDER[0] * H
         load_activations(0)
         load_embeddings(0)
         load_ws(0)
         load_words(0, 0)
-        load_scales(0, N_TILE)
+        load_scales(first_column, first_column + N_TILE)
         load_activations(1)
-        load_scales(N_TILE, H)
+        load_scales(first_column + N_TILE, first_column + H)
         load_words(0, 1)
         load_embeddings(1)
-        for bt in range(2, B_TILES):
-            load_activations(bt)
-            load_embeddings(bt)
-        load_scales(H, G * H)
+        load_activations(2)
+        load_embeddings(2)
         load_ws(1)
+        load_activations(3)
+        load_embeddings(3)
+        load_gate_scales(1)
         for half in range(HALVES):
             load_words(1, half)
         c_raw = const.tile([P, B_TILES, H], BF16)
@@ -202,7 +208,8 @@ def tile_hyperlstmcell_pb_kernel(
                             flipped[:, g, u, :], words[:, 256 * g + u : 256 * (g + 1) : 2], ident_f32[:]
                         )
                 together = work.tile([P, PASSES * P * 4], BF16, name="grouped%d" % operand, bufs=1, align_bytes=64)
-                nc.vector.tensor_copy(
+                copy_out = nc.vector.tensor_copy if bt == 0 else nc.scalar.copy
+                copy_out(
                     out=together[:].bitcast(F32).rearrange("p (g b u) -> p g b u", g=PASSES, u=2),
                     in_=flipped[:].rearrange("p g u b -> p g b u"),
                 )
@@ -433,16 +440,14 @@ def tile_hyperlstmcell_pb_kernel(
                     out=acted[job][:, blocks(half)], in0=acted[job][:, blocks(half)], in1=c_t[:, bt, blocks(half)], op=ALU.mult
                 )
 
-        def cell_sum(job, half):
-            bt = job % B_TILES
-            nc.vector.tensor_tensor(
-                out=state[bt][:, blocks(half)], in0=state[bt][:, blocks(half)], in1=acted[job][:, blocks(half)], op=ALU.add
-            )
-
-        def unflip(name, source, bt, half):
+        def unflip(name, sources, bt, half):
             bank = flip_bank([P, BANK_BLOCKS, P], F32)
             for j in range(BANK_BLOCKS):
-                nc.tensor.transpose(bank[:, j, :], source[:, half * BANK_BLOCKS + j, :], ident_f32[:])
+                for i, source in enumerate(sources):
+                    nc.tensor.matmul(
+                        out=bank[:, j, :], lhsT=source[:, half * BANK_BLOCKS + j, :], rhs=ident_f32[:], is_transpose=True,
+                        start=(i == 0), stop=(i == len(sources) - 1),
+                    )
             returned[(name, bt, half)] = bank
 
         def cell_out(bt, half):
@@ -539,9 +544,6 @@ def tile_hyperlstmcell_pb_kernel(
             due = half_due(k, LAG_NORMALISE, every_gate)
             if due is not None:
                 normalise(due[0], due[1])
-            due = half_due(k, LAG_CELL, (GATE_F,))
-            if due is not None:
-                cell_sum(due[0], due[1])
             due = half_due(k, LAG_CELL_NORMALISE, (GATE_F,))
             if due is not None:
                 centre_times_gamma(cell_key(due[0]), cell[due[0] % B_TILES], gamma_c, due[1])
@@ -554,26 +556,28 @@ def tile_hyperlstmcell_pb_kernel(
                 times_rstd_plus_beta(cell_key(due[0]), cell[bt], beta_c, due[1])
                 nc.sync.dma_start(out=out_1[bt * P : (bt + 1) * P, columns(due[1])], in_=cell[bt][:, columns(due[1])])
 
+            if position == 1 and step < B_TILES:
+                flip_c(step)
+            if 4 <= step < 7 and position < G - 1:
+                flip_ws(position + 1, step - 4)
+
             due = half_due(k, LAG_FLIP, every_gate)
             if due is not None:
                 flip(due[0], due[1])
             due = half_due(k, LAG_UNFLIP, (GATE_F,))
             if due is not None:
-                unflip("cell", state[due[0] % B_TILES], due[0] % B_TILES, due[1])
+                unflip("cell", (state[due[0] % B_TILES], acted[due[0]]), due[0] % B_TILES, due[1])
             due = half_due(k, LAG_RETURN, (GATE_O,))
             if due is not None:
-                unflip("o", acted[due[0]], due[0] % B_TILES, due[1])
+                unflip("o", (acted[due[0]],), due[0] % B_TILES, due[1])
 
             if k // 2 + 1 < B_TILES:
                 if k % 2 == 0:
                     prepare_activations(k // 2 + 1)
                 else:
                     prepare_embeddings(k // 2 + 1)
-            if position == 1 and step < B_TILES:
-                flip_c(step)
             if step == 1 and 1 <= position < G - 1:
                 load_ws(position + 1)
+                load_gate_scales(position + 1)
                 for half in range(HALVES):
                     load_words(position + 1, half)
-            if 4 <= step < 7 and position < G - 1:
-                flip_ws(position + 1, step - 4)

@@ -47,12 +47,12 @@ LAG_OUTPUT = 9
 LAG_UNFLIP = 9
 LAG_CELL_OUT = 10
 LAG_CELL_MEAN = 12
-LAG_CELL_SQUARE = 13
-LAG_CELL_ROOT = 14
-LAG_CELL_NORMALISE = 14
-LAG_CELL_RSTD = 15
-LAG_CELL_SHIFT = 15
-LAG_CELL_TANH = 16
+LAG_CELL_SQUARE = 12
+LAG_CELL_ROOT = 13
+LAG_CELL_NORMALISE = 13
+LAG_CELL_RSTD = 14
+LAG_CELL_SHIFT = 14
+LAG_CELL_TANH = 15
 LAST_LAG = LAG_CELL_TANH + 1
 
 FLOPS = 2 * 2 * B * K * G * H + 3 * 2 * B * G * H * E

@@ -94,7 +94,7 @@ def tile_hyperlstmcell_pb_kernel(
         def flip_bank(shape, dtype):
             return psum.tile(shape, dtype, name="flip", bufs=3)
 
-        planes = const.tile([P, G * H], U8, align_bytes=64)
+        planes = const.tile([P, G * H], U8, align_bytes=256)
         nc.vector.memset(planes[:].bitcast(I32), 0)
         one_half = const.tile([P, 1], F32)
         nc.vector.memset(one_half[:], 0.5)
@@ -139,7 +139,7 @@ def tile_hyperlstmcell_pb_kernel(
         def load_words(position, half):
             gate = GATE_ORDER[position]
             if half == 0:
-                w_words[position] = per_gate.tile([P, 2, PASSES, H], U32, name="w_words", align_bytes=64)
+                w_words[position] = per_gate.tile([P, 2, PASSES, H], U32, name="w_words", align_bytes=256)
             first_unit = gate * H + half * N_TILE
             for operand, source in enumerate((Wih_words, Whh_words)):
                 for g in range(PASSES):
@@ -193,8 +193,8 @@ def tile_hyperlstmcell_pb_kernel(
         beta_c = const.tile([P, H], BF16)
         nc.sync.dma_start(out=beta_c[:], in_=lnc_beta.partition_broadcast(P))
 
-        act_codes = const.tile([P, 2, B_TILES, PASSES, P], U32, align_bytes=64)
-        act_scales = const.tile([P, 2, B_TILES, PASSES, P], U8, align_bytes=64)
+        act_codes = const.tile([P, 2, B_TILES, PASSES, P], U32, align_bytes=256)
+        act_scales = const.tile([P, 2, B_TILES, PASSES, P], U8, align_bytes=256)
         emb_t = [const.tile([P, G, B], BF16, name="emb_t%d" % i) for i in range(3)]
 
         def prepare_activations(bt):

@@ -35,22 +35,22 @@ JOBS = G * B_TILES
 SLOTS = JOBS * HALVES
 
 LAG_MEAN = 2
-LAG_SQUARE = 3
+LAG_SQUARE = 4
 LAG_ROOT = 4
 LAG_RSTD = 5
-LAG_NORMALISE = 5
-LAG_FLIP = 6
+LAG_NORMALISE = 6
+LAG_FLIP = 7
 LAG_ACTIVATE = 7
 LAG_CELL = 8
 LAG_RETURN = 8
 LAG_OUTPUT = 9
-LAG_UNFLIP = 9
-LAG_CELL_OUT = 10
-LAG_CELL_MEAN = 12
-LAG_CELL_SQUARE = 12
-LAG_CELL_ROOT = 13
-LAG_CELL_NORMALISE = 13
-LAG_CELL_RSTD = 14
+LAG_UNFLIP = 8
+LAG_CELL_OUT = 8
+LAG_CELL_MEAN = 10
+LAG_CELL_SQUARE = 11
+LAG_CELL_ROOT = 11
+LAG_CELL_NORMALISE = 12
+LAG_CELL_RSTD = 13
 LAG_CELL_SHIFT = 14
 LAG_CELL_TANH = 15
 LAST_LAG = LAG_CELL_TANH + 1
@@ -274,24 +274,24 @@ def tile_hyperlstmcell_pb_kernel(
         def columns(half):
             return slice(half * N_TILE, (half + 1) * N_TILE)
 
-        def matmuls(k):
+        def plain_matmul(k, i, tag):
             job, half = divmod(k, HALVES)
             position, bt = divmod(job, B_TILES)
             gate = GATE_ORDER[position]
-            samples = slice(bt * P, (bt + 1) * P)
-            def plain_matmuls(plain):
-                for i, tag in plain:
-                    z = psum.tile([P, N_TILE], F32, name=tag)
-                    with_bias = tag == "zb" and position > 0
-                    nc.tensor.matmul(
-                        out=z[:], lhsT=emb_t[i][:, gate, samples], rhs=ws_t[position][i][:, columns(half)],
-                        start=True, stop=not with_bias,
-                    )
-                    if with_bias:
-                        nc.tensor.matmul(out=z[:], lhsT=row_picker(gate, half), rhs=rows[:], start=False, stop=True)
-                    banks[tag] = z
+            z = psum.tile([P, N_TILE], F32, name=tag)
+            with_bias = tag == "zb" and position > 0
+            nc.tensor.matmul(
+                out=z[:], lhsT=emb_t[i][:, gate, bt * P : (bt + 1) * P], rhs=ws_t[position][i][:, columns(half)],
+                start=True, stop=not with_bias,
+            )
+            if with_bias:
+                nc.tensor.matmul(out=z[:], lhsT=row_picker(gate, half), rhs=rows[:], start=False, stop=True)
+            banks[tag] = z
 
-            plain_matmuls(((0, "zx"), (1, "zh")))
+        def mx_matmuls(k):
+            job, half = divmod(k, HALVES)
+            position, bt = divmod(job, B_TILES)
+            gate = GATE_ORDER[position]
             for operand, tag in enumerate(("xh", "hh")):
                 acc = psum.tile([P, N_TILE], F32, name=tag)
                 for g in range(PASSES):
@@ -306,7 +306,6 @@ def tile_hyperlstmcell_pb_kernel(
                         stop=(g == PASSES - 1),
                     )
                 banks[tag] = acc
-            plain_matmuls(((2, "zb"),))
             if half == 0:
                 pre[job] = jobs.tile([P, H], F32, name="pre")
                 stats[job] = {"parts": small.tile([P, 2 * HALVES], F32, name="parts")}
@@ -374,10 +373,10 @@ def tile_hyperlstmcell_pb_kernel(
             nc.vector.reciprocal(out=rstd[:], in_=stats[key]["padded"][:])
             stats[key]["rstd"] = rstd
 
-        def centre_times_gamma(key, values, gamma_row, half):
+        def centre_times_gamma(key, values, gamma_row):
             nc.vector.scalar_tensor_tensor(
-                out=values[:, columns(half)], in0=values[:, columns(half)], scalar=stats[key]["minus_mean"][:, 0:1],
-                in1=gamma_row[:, columns(half)], op0=ALU.add, op1=ALU.mult,
+                out=values[:], in0=values[:], scalar=stats[key]["minus_mean"][:, 0:1], in1=gamma_row[:],
+                op0=ALU.add, op1=ALU.mult,
             )
 
         def times_rstd_plus_beta(key, values, beta_row, half):
@@ -393,9 +392,9 @@ def tile_hyperlstmcell_pb_kernel(
         cell = [None] * B_TILES
         tanh_c = [None] * B_TILES
 
-        def normalise(job, half):
+        def normalise(job):
             nc.vector.tensor_scalar(
-                out=pre[job][:, columns(half)], in0=pre[job][:, columns(half)],
+                out=pre[job][:], in0=pre[job][:],
                 scalar1=stats[job]["minus_mean"][:, 0:1], scalar2=stats[job]["rstd"][:, 0:1],
                 op0=ALU.add, op1=ALU.mult,
             )
@@ -429,16 +428,15 @@ def tile_hyperlstmcell_pb_kernel(
         def blocks(half):
             return slice(half * BANK_BLOCKS, (half + 1) * BANK_BLOCKS)
 
-        def cell_product(job, half):
+        def input_product(job):
             bt = job % B_TILES
-            if gate_of(job) == GATE_G:
-                nc.vector.tensor_tensor(
-                    out=state[bt][:, blocks(half)], in0=state[bt][:, blocks(half)], in1=acted[job][:, blocks(half)], op=ALU.mult
-                )
-            if gate_of(job) == GATE_F:
-                nc.vector.tensor_tensor(
-                    out=acted[job][:, blocks(half)], in0=acted[job][:, blocks(half)], in1=c_t[:, bt, blocks(half)], op=ALU.mult
-                )
+            nc.vector.tensor_tensor(out=state[bt][:], in0=state[bt][:], in1=acted[job][:], op=ALU.mult)
+
+        def forget_product(job, half):
+            bt = job % B_TILES
+            nc.vector.tensor_tensor(
+                out=acted[job][:, blocks(half)], in0=acted[job][:, blocks(half)], in1=c_t[:, bt, blocks(half)], op=ALU.mult
+            )
 
         def unflip(name, sources, bt, half):
             bank = flip_bank([P, BANK_BLOCKS, P], F32)
@@ -490,10 +488,10 @@ def tile_hyperlstmcell_pb_kernel(
             return ("cell", job % B_TILES)
 
         def small_step(k, gate_lag, cell_lag, step):
-            job = job_due(k, gate_lag, every_gate)
+            job = None if gate_lag is None else job_due(k, gate_lag, every_gate)
             if job is not None:
                 step(job)
-            job = job_due(k, cell_lag, (GATE_F,))
+            job = None if cell_lag is None else job_due(k, cell_lag, (GATE_F,))
             if job is not None:
                 step(cell_key(job))
 
@@ -507,69 +505,78 @@ def tile_hyperlstmcell_pb_kernel(
         slots_a_gate = SLOTS // G
         for k in range(SLOTS + LAST_LAG + 1):
             position, step = divmod(k, slots_a_gate)
-            if k < SLOTS:
-                job, half = divmod(k, HALVES)
-                matmuls(k)
-                copy_z(k)
-                leave_psum("xh", terms["zx"][:], ALU.mult)
-            small_step(k, LAG_MEAN, LAG_CELL_MEAN, norm_mean)
-            small_step(k, LAG_ROOT, LAG_CELL_ROOT, norm_root)
-            if k < SLOTS:
-                if position == 0:
-                    leave_psum("zb", first_bias[:, columns(half)], ALU.add)
-                product_h(k)
-            small_step(k, LAG_RSTD, LAG_CELL_RSTD, norm_rstd)
-            if k < SLOTS:
-                sum_terms(k)
+            issues = k < SLOTS
+            half = k % HALVES
 
-            due = half_due(k, LAG_ACTIVATE, every_gate)
+            due = half_due(k, LAG_FLIP, every_gate)
             if due is not None:
-                activate(due[0], due[1])
-            job_to_square = job_due(k, LAG_SQUARE, every_gate)
-            if job_to_square is not None:
-                square_job(job_to_square, pre[job_to_square])
-            due = half_due(k, LAG_CELL_OUT, (GATE_F,))
-            if due is not None:
-                cell_out(due[0] % B_TILES, due[1])
-            job_to_square = job_due(k, LAG_CELL_SQUARE, (GATE_F,))
-            if job_to_square is not None:
-                square_job(cell_key(job_to_square), cell[job_to_square % B_TILES])
-            due = half_due(k, LAG_CELL_TANH, (GATE_F,))
-            if due is not None:
-                cell_tanh(due[0] % B_TILES, due[1])
-
-            due = half_due(k, LAG_CELL, (GATE_G, GATE_F))
-            if due is not None:
-                cell_product(due[0], due[1])
-            due = half_due(k, LAG_NORMALISE, every_gate)
-            if due is not None:
-                normalise(due[0], due[1])
-            due = half_due(k, LAG_CELL_NORMALISE, (GATE_F,))
-            if due is not None:
-                centre_times_gamma(cell_key(due[0]), cell[due[0] % B_TILES], gamma_c, due[1])
+                flip(due[0], due[1])
             due = half_due(k, LAG_OUTPUT, (GATE_O,))
             if due is not None:
                 output(due[0], due[1])
-            due = half_due(k, LAG_CELL_SHIFT, (GATE_F,))
+            due = half_due(k, LAG_CELL, (GATE_F,))
             if due is not None:
-                bt = due[0] % B_TILES
-                times_rstd_plus_beta(cell_key(due[0]), cell[bt], beta_c, due[1])
-                nc.sync.dma_start(out=out_1[bt * P : (bt + 1) * P, columns(due[1])], in_=cell[bt][:, columns(due[1])])
+                forget_product(due[0], due[1])
+            job = job_due(k, LAG_CELL + 1, (GATE_G,))
+            if job is not None:
+                input_product(job)
+            job = job_due(k, LAG_NORMALISE, every_gate)
+            if job is not None:
+                normalise(job)
 
+            if issues:
+                plain_matmul(k, 0, "zx")
+                plain_matmul(k, 1, "zh")
+                copy_z(k)
+                mx_matmuls(k)
+            job = job_due(k, LAG_SQUARE, every_gate)
+            if job is not None:
+                square_job(job, pre[job])
+            due = half_due(k, LAG_ACTIVATE, every_gate)
+            if due is not None:
+                activate(due[0], due[1])
+            job = job_due(k, LAG_CELL_SQUARE, (GATE_F,))
+            if job is not None:
+                square_job(cell_key(job), cell[job % B_TILES])
+            due = half_due(k, LAG_CELL_TANH, (GATE_F,))
+            if due is not None:
+                cell_tanh(due[0] % B_TILES, due[1])
+            small_step(k, None, LAG_CELL_MEAN, norm_mean)
+            if issues:
+                leave_psum("xh", terms["zx"][:], ALU.mult)
+                product_h(k)
+                plain_matmul(k, 2, "zb")
+
+            due = half_due(k, LAG_RETURN, (GATE_O,))
+            if due is not None:
+                unflip("o", (acted[due[0]],), due[0] % B_TILES, due[1])
             if position == 1 and step < B_TILES:
                 flip_c(step)
             if 4 <= step < 7 and position < G - 1:
                 flip_ws(position + 1, step - 4)
 
-            due = half_due(k, LAG_FLIP, every_gate)
+            small_step(k, LAG_MEAN, None, norm_mean)
+            small_step(k, LAG_RSTD, LAG_CELL_RSTD, norm_rstd)
+            small_step(k, LAG_ROOT, LAG_CELL_ROOT, norm_root)
+            due = half_due(k, LAG_CELL_SHIFT, (GATE_F,))
             if due is not None:
-                flip(due[0], due[1])
+                bt = due[0] % B_TILES
+                times_rstd_plus_beta(cell_key(due[0]), cell[bt], beta_c, due[1])
+                nc.sync.dma_start(out=out_1[bt * P : (bt + 1) * P, columns(due[1])], in_=cell[bt][:, columns(due[1])])
+            if issues:
+                if position == 0:
+                    leave_psum("zb", first_bias[:, columns(half)], ALU.add)
+                sum_terms(k)
+
             due = half_due(k, LAG_UNFLIP, (GATE_F,))
             if due is not None:
                 unflip("cell", (state[due[0] % B_TILES], acted[due[0]]), due[0] % B_TILES, due[1])
-            due = half_due(k, LAG_RETURN, (GATE_O,))
+            due = half_due(k, LAG_CELL_OUT, (GATE_F,))
             if due is not None:
-                unflip("o", (acted[due[0]],), due[0] % B_TILES, due[1])
+                cell_out(due[0] % B_TILES, due[1])
+            job = job_due(k, LAG_CELL_NORMALISE, (GATE_F,))
+            if job is not None:
+                centre_times_gamma(cell_key(job), cell[job % B_TILES], gamma_c)
 
             if k // 2 + 1 < B_TILES:
                 if k % 2 == 0:

@@ -148,12 +148,13 @@ def tile_hyperlstmcell_pb_kernel(
                         in_=source[g, :, first_unit : first_unit + N_TILE, :].rearrange("p n t -> p (n t)").bitcast(I32),
                     )
 
-        nc.gpsimd.dma_start(out=rows[0 : G * HALVES, :], in_=bias.rearrange("(r n) -> r n", n=N_TILE))
-        for i, source in enumerate((ln_gamma, ln_beta)):
-            nc.gpsimd.dma_start(
-                out=norm_rows[i * G * UNIT_BLOCKS : (i + 1) * G * UNIT_BLOCKS, :],
-                in_=source.rearrange("g (j p) -> (g j) p", p=P),
-            )
+        def load_small_vectors():
+            nc.sync.dma_start(out=rows[0 : G * HALVES, :], in_=bias.rearrange("(r n) -> r n", n=N_TILE))
+            for i, source in enumerate((ln_gamma, ln_beta)):
+                nc.sync.dma_start(
+                    out=norm_rows[i * G * UNIT_BLOCKS : (i + 1) * G * UNIT_BLOCKS, :],
+                    in_=source.rearrange("g (j p) -> (g j) p", p=P),
+                )
 
         def load_scales(first_column, last_column):
             for operand, source in enumerate((Wih_scales, Whh_scales)):
@@ -172,10 +173,10 @@ def tile_hyperlstmcell_pb_kernel(
         load_activations(0)
         load_embeddings(0)
         load_ws(0)
+        load_scales(first_column, first_column + H)
         load_words(0, 0)
-        load_scales(first_column, first_column + N_TILE)
+        load_small_vectors()
         load_activations(1)
-        load_scales(first_column + N_TILE, first_column + H)
         load_words(0, 1)
         load_embeddings(1)
         load_activations(2)
@@ -499,8 +500,6 @@ def tile_hyperlstmcell_pb_kernel(
         prepare_embeddings(0)
         for i in range(3):
             flip_ws(0, i)
-        spread_first_bias()
-        flip_norm_rows()
 
         slots_a_gate = SLOTS // G
         for k in range(SLOTS + LAST_LAG + 1):
@@ -529,6 +528,10 @@ def tile_hyperlstmcell_pb_kernel(
                 plain_matmul(k, 1, "zh")
                 copy_z(k)
                 mx_matmuls(k)
+            if k == 0:
+                spread_first_bias()
+            if k == 2:
+                flip_norm_rows()
             job = job_due(k, LAG_SQUARE, every_gate)
             if job is not None:
                 square_job(job, pre[job])

@@ -94,6 +94,8 @@ def tile_hyperlstmcell_pb_kernel(
         def flip_bank(shape, dtype):
             return psum.tile(shape, dtype, name="flip", bufs=3)
 
+        zeros = const.tile([P, P], F32)
+        nc.vector.memset(zeros[:], 0.0)
         planes = const.tile([P, G * H], U8, align_bytes=256)
         nc.vector.memset(planes[:].bitcast(I32), 0)
         one_half = const.tile([P, 1], F32)
@@ -196,7 +198,7 @@ def tile_hyperlstmcell_pb_kernel(
 
         act_codes = const.tile([P, 2, B_TILES, PASSES, P], U32, align_bytes=256)
         act_scales = const.tile([P, 2, B_TILES, PASSES, P], U8, align_bytes=256)
-        emb_t = [const.tile([P, G, B], BF16, name="emb_t%d" % i) for i in range(3)]
+        emb_t = [const.tile([P, 3, G, P], BF16, name="emb_t%d" % bt) for bt in range(B_TILES)]
 
         def prepare_activations(bt):
             grouped = []
@@ -227,7 +229,7 @@ def tile_hyperlstmcell_pb_kernel(
                 emb_flip = flip_bank([P, G, P], BF16)
                 for gate in range(G):
                     nc.tensor.transpose(emb_flip[:, gate, :], emb_raw[bt][:, i, gate * E : (gate + 1) * E], ident_bf[:])
-                nc.scalar.copy(out=emb_t[i][:, :, bt * P : (bt + 1) * P], in_=emb_flip[:])
+                nc.scalar.copy(out=emb_t[bt][:, i], in_=emb_flip[:])
 
         def flip_ws(position, i):
             ws_flip = flip_bank([P, UNIT_BLOCKS, P], BF16)
@@ -251,11 +253,11 @@ def tile_hyperlstmcell_pb_kernel(
             r = gate * HALVES + half
             return ident_bf[:, r : r + 1].to_broadcast([P, P])
 
-        def spread_first_bias():
-            for half, copy_out in enumerate((nc.scalar.copy, nc.vector.tensor_copy)):
-                repeated = flip_bank([P, N_TILE], F32)
-                nc.tensor.matmul(out=repeated[:], lhsT=row_picker(GATE_ORDER[0], half), rhs=rows[:], start=True, stop=True)
-                copy_out(out=first_bias[:, half * N_TILE : (half + 1) * N_TILE], in_=repeated[:])
+        def spread_first_bias(half):
+            repeated = flip_bank([P, N_TILE], F32)
+            nc.tensor.matmul(out=repeated[:], lhsT=row_picker(GATE_ORDER[0], half), rhs=rows[:], start=True, stop=True)
+            copy_out = nc.scalar.copy if half == 0 else nc.vector.tensor_copy
+            copy_out(out=first_bias[:, half * N_TILE : (half + 1) * N_TILE], in_=repeated[:])
 
         norm_cols = const.tile([P, 2 * G * UNIT_BLOCKS], F32)
 
@@ -282,7 +284,7 @@ def tile_hyperlstmcell_pb_kernel(
             z = psum.tile([P, N_TILE], F32, name=tag)
             with_bias = tag == "zb" and position > 0
             nc.tensor.matmul(
-                out=z[:], lhsT=emb_t[i][:, gate, bt * P : (bt + 1) * P], rhs=ws_t[position][i][:, columns(half)],
+                out=z[:], lhsT=emb_t[bt][:, i, gate, :], rhs=ws_t[position][i][:, columns(half)],
                 start=True, stop=not with_bias,
             )
             if with_bias:
@@ -496,9 +498,18 @@ def tile_hyperlstmcell_pb_kernel(
             if job is not None:
                 step(cell_key(job))
 
+        idle = psum.tile([P, P], F32, name="xh")
+
+        def keep_clock(count):
+            for repeat in range(count):
+                nc.tensor.matmul(out=idle[:], lhsT=zeros[:], rhs=zeros[:], start=True, stop=True)
+
+        keep_clock(5)
         prepare_activations(0)
+        keep_clock(1)
         prepare_embeddings(0)
         for i in range(3):
+            keep_clock(1)
             flip_ws(0, i)
 
         slots_a_gate = SLOTS // G
@@ -529,7 +540,7 @@ def tile_hyperlstmcell_pb_kernel(
                 copy_z(k)
                 mx_matmuls(k)
             if k == 0:
-                spread_first_bias()
+                spread_first_bias(0)
             if k == 2:
                 flip_norm_rows()
             job = job_due(k, LAG_SQUARE, every_gate)
@@ -558,18 +569,21 @@ def tile_hyperlstmcell_pb_kernel(
             if 4 <= step < 7 and position < G - 1:
                 flip_ws(position + 1, step - 4)
 
-            small_step(k, LAG_MEAN, None, norm_mean)
-            small_step(k, LAG_RSTD, LAG_CELL_RSTD, norm_rstd)
-            small_step(k, LAG_ROOT, LAG_CELL_ROOT, norm_root)
             due = half_due(k, LAG_CELL_SHIFT, (GATE_F,))
             if due is not None:
                 bt = due[0] % B_TILES
                 times_rstd_plus_beta(cell_key(due[0]), cell[bt], beta_c, due[1])
                 nc.sync.dma_start(out=out_1[bt * P : (bt + 1) * P, columns(due[1])], in_=cell[bt][:, columns(due[1])])
+            small_step(k, LAG_MEAN, None, norm_mean)
+            small_step(k, LAG_RSTD, LAG_CELL_RSTD, norm_rstd)
+            small_step(k, LAG_ROOT, LAG_CELL_ROOT, norm_root)
             if issues:
                 if position == 0:
                     leave_psum("zb", first_bias[:, columns(half)], ALU.add)
                 sum_terms(k)
+
+            if k == 0:
+                spread_first_bias(1)
 
             due = half_due(k, LAG_UNFLIP, (GATE_F,))
             if due is not None:

@@ -189,6 +189,10 @@ def tile_hyperlstmcell_pb_kernel(
         load_gate_scales(1)
         for half in range(HALVES):
             load_words(1, half)
+        bias_spread = [const.tile([P, H], BF16, name="bias_spread%d" % position) for position in range(2)]
+
+        second_gate = GATE_ORDER[1] * H
+        nc.sync.dma_start(out=bias_spread[1][:], in_=bias[second_gate : second_gate + H].partition_broadcast(P))
         c_raw = const.tile([P, B_TILES, H], BF16)
         nc.sync.dma_start(out=c_raw[:], in_=c.rearrange("(t p) n -> p t n", p=P))
         gamma_c = const.tile([P, H], BF16)
@@ -247,7 +251,9 @@ def tile_hyperlstmcell_pb_kernel(
                 nc.tensor.transpose(c_flip[:, j, :], c_raw[:, bt, j * P : (j + 1) * P], ident_bf[:])
             nc.scalar.copy(out=c_t[:, bt], in_=c_flip[:])
 
-        first_bias = const.tile([P, H], BF16)
+        def bias_by_vector(k):
+            job, half = divmod(k, HALVES)
+            return job < B_TILES or (job < 2 * B_TILES and half == 0)
 
         def row_picker(gate, half):
             r = gate * HALVES + half
@@ -257,7 +263,7 @@ def tile_hyperlstmcell_pb_kernel(
             repeated = flip_bank([P, N_TILE], F32)
             nc.tensor.matmul(out=repeated[:], lhsT=row_picker(GATE_ORDER[0], half), rhs=rows[:], start=True, stop=True)
             copy_out = nc.scalar.copy if half == 0 else nc.vector.tensor_copy
-            copy_out(out=first_bias[:, half * N_TILE : (half + 1) * N_TILE], in_=repeated[:])
+            copy_out(out=bias_spread[0][:, half * N_TILE : (half + 1) * N_TILE], in_=repeated[:])
 
         norm_cols = const.tile([P, 2 * G * UNIT_BLOCKS], F32)
 
@@ -282,7 +288,7 @@ def tile_hyperlstmcell_pb_kernel(
             position, bt = divmod(job, B_TILES)
             gate = GATE_ORDER[position]
             z = psum.tile([P, N_TILE], F32, name=tag)
-            with_bias = tag == "zb" and position > 0
+            with_bias = tag == "zb" and not bias_by_vector(k)
             nc.tensor.matmul(
                 out=z[:], lhsT=emb_t[bt][:, i, gate, :], rhs=ws_t[position][i][:, columns(half)],
                 start=True, stop=not with_bias,
@@ -337,7 +343,7 @@ def tile_hyperlstmcell_pb_kernel(
         def sum_terms(k):
             job, half = divmod(k, HALVES)
             parts = stats[job]["parts"]
-            shift = terms["zb"] if job < B_TILES else banks["zb"]
+            shift = terms["zb"] if bias_by_vector(k) else banks["zb"]
             nc.vector.scalar_tensor_tensor(
                 out=terms["xh"][:], in0=shift[:], scalar=1.0, in1=terms["xh"][:], op0=ALU.mult, op1=ALU.add,
                 accum_out=parts[:, 2 * half + 1 : 2 * half + 2],
@@ -469,11 +475,16 @@ def tile_hyperlstmcell_pb_kernel(
 
         def output(job, half):
             bt = job % B_TILES
-            nc.vector.tensor_tensor(
-                out=tanh_c[bt][:, columns(half)], in0=returned[("o", bt, half)][:].rearrange("p j n -> p (j n)"),
-                in1=tanh_c[bt][:, columns(half)], op=ALU.mult,
-            )
-            nc.sync.dma_start(out=out_0[bt * P : (bt + 1) * P, columns(half)], in_=tanh_c[bt][:, columns(half)])
+            pieces = 2 if job == JOBS - 1 and half == HALVES - 1 else 1
+            width = N_TILE // pieces
+            bank = returned[("o", bt, half)][:].rearrange("p j n -> p (j n)")
+            for piece in range(pieces):
+                piece_columns = slice(half * N_TILE + piece * width, half * N_TILE + (piece + 1) * width)
+                nc.vector.tensor_tensor(
+                    out=tanh_c[bt][:, piece_columns], in0=bank[:, piece * width : (piece + 1) * width],
+                    in1=tanh_c[bt][:, piece_columns], op=ALU.mult,
+                )
+                nc.sync.dma_start(out=out_0[bt * P : (bt + 1) * P, piece_columns], in_=tanh_c[bt][:, piece_columns])
 
         every_gate = GATE_ORDER
 
@@ -578,8 +589,8 @@ def tile_hyperlstmcell_pb_kernel(
             small_step(k, LAG_RSTD, LAG_CELL_RSTD, norm_rstd)
             small_step(k, LAG_ROOT, LAG_CELL_ROOT, norm_root)
             if issues:
-                if position == 0:
-                    leave_psum("zb", first_bias[:, columns(half)], ALU.add)
+                if bias_by_vector(k):
+                    leave_psum("zb", bias_spread[position][:, columns(half)], ALU.add)
                 sum_terms(k)
 
             if k == 0:

@@ -55,6 +55,9 @@ LAG_CELL_SHIFT = 14
 LAG_CELL_TANH = 15
 LAST_LAG = LAG_CELL_TANH + 1
 
+WS_STEPS = (3, 5, 7)
+FIRST_WS_STEPS = (4, 6, 7)
+
 FLOPS = 2 * 2 * B * K * G * H + 3 * 2 * B * G * H * E
 
 
@@ -577,8 +580,9 @@ def tile_hyperlstmcell_pb_kernel(
                 unflip("o", (acted[due[0]],), due[0] % B_TILES, due[1])
             if position == 1 and step < B_TILES:
                 flip_c(step)
-            if 4 <= step < 7 and position < G - 1:
-                flip_ws(position + 1, step - 4)
+            ws_steps = FIRST_WS_STEPS if position == 0 else WS_STEPS
+            if step in ws_steps and position < G - 1:
+                flip_ws(position + 1, ws_steps.index(step))
 
             due = half_due(k, LAG_CELL_SHIFT, (GATE_F,))
             if due is not None:

@@ -520,7 +520,7 @@ def tile_hyperlstmcell_pb_kernel(
 
         keep_clock(5)
         prepare_activations(0)
-        keep_clock(1)
+        keep_clock(2)
         prepare_embeddings(0)
         for i in range(3):
             keep_clock(1)
@@ -609,6 +609,11 @@ def tile_hyperlstmcell_pb_kernel(
             job = job_due(k, LAG_CELL_NORMALISE, (GATE_F,))
             if job is not None:
                 centre_times_gamma(cell_key(job), cell[job % B_TILES], gamma_c)
+
+            if k == SLOTS:
+                idle = psum.tile([P, P], F32, name="xh")
+            if SLOTS <= k < SLOTS + LAG_RETURN:
+                keep_clock(2)
 
             if k // 2 + 1 < B_TILES:
                 if k % 2 == 0:

from contextlib import ExitStack

import concourse.mybir as mybir
from concourse.masks import make_identity

F32 = mybir.dt.float32
BF16 = mybir.dt.bfloat16
U32 = mybir.dt.uint32
U8 = mybir.dt.uint8
I32 = mybir.dt.int32
FP8X4 = mybir.dt.float8_e4m3fn_x4
ALU = mybir.AluOpType
ACT = mybir.ActivationFunctionType
AXIS = mybir.AxisListType

P = 128
B = 512
K = 1024
H = 1024
G = 4
E = 128
EPS = 1e-6

B_TILES = B // P
K_PASS = 4 * P
PASSES = K // K_PASS
N_TILE = 512
HALVES = H // N_TILE
UNIT_BLOCKS = H // P
BANK_BLOCKS = N_TILE // P

GATE_I, GATE_F, GATE_G, GATE_O = 0, 1, 2, 3
GATE_ORDER = (GATE_I, GATE_G, GATE_F, GATE_O)
JOBS = G * B_TILES
SLOTS = JOBS * HALVES

LAG_MEAN = 2
LAG_SQUARE = 4
LAG_ROOT = 4
LAG_RSTD = 5
LAG_NORMALISE = 6
LAG_FLIP = 7
LAG_ACTIVATE = 7
LAG_CELL = 8
LAG_RETURN = 8
LAG_OUTPUT = 9
LAG_UNFLIP = 8
LAG_CELL_OUT = 8
LAG_CELL_MEAN = 10
LAG_CELL_SQUARE = 11
LAG_CELL_ROOT = 11
LAG_CELL_NORMALISE = 12
LAG_CELL_RSTD = 13
LAG_CELL_SHIFT = 14
LAG_CELL_TANH = 15
LAST_LAG = LAG_CELL_TANH + 1

WS_STEPS = (3, 5, 7)
FIRST_WS_STEPS = (4, 6, 7)

FLOPS = 2 * 2 * B * K * G * H + 3 * 2 * B * G * H * E


def tile_hyperlstmcell_pb_kernel(
    tc,
    x,
    h,
    c,
    emb_h,
    emb_x,
    emb_b,
    Wsh,
    Wsx,
    Wsb,
    Wih_words,
    Wih_scales,
    Whh_words,
    Whh_scales,
    bias,
    ln_gamma,
    ln_beta,
    lnc_gamma,
    lnc_beta,
    out_0,
    out_1,
):
    nc = tc.nc
    with ExitStack() as ctx:
        ctx.enter_context(tc.manual_schedule())
        const = ctx.enter_context(tc.tile_pool(name="const", bufs=1))
        per_gate = ctx.enter_context(tc.tile_pool(name="per_gate", bufs=2))
        work = ctx.enter_context(tc.tile_pool(name="work", bufs=3))
        jobs = ctx.enter_context(tc.tile_pool(name="jobs", bufs=4))
        small = ctx.enter_context(tc.tile_pool(name="small", bufs=8))
        psum = ctx.enter_context(tc.psum_pool(name="psum", bufs=1))

        def flip_bank(shape, dtype):
            return psum.tile(shape, dtype, name="flip", bufs=3)

        zeros = const.tile([P, P], F32)
        nc.vector.memset(zeros[:], 0.0)
        planes = const.tile([P, G * H], U8, align_bytes=256)
        nc.vector.memset(planes[:].bitcast(I32), 0)
        one_half = const.tile([P, 1], F32)
        nc.vector.memset(one_half[:], 0.5)
        rows = const.tile([P, N_TILE], BF16)
        nc.vector.memset(rows[:], 0.0)
        norm_rows = const.tile([P, P], BF16)
        nc.vector.memset(norm_rows[:], 0.0)
        warm = const.tile([P, 1], F32)
        nc.scalar.activation(out=warm[:], in_=one_half[:], func=ACT.Sigmoid)
        ident_f32 = const.tile([P, P], F32)
        make_identity(nc, ident_f32[:])
        ident_bf = const.tile([P, P], BF16)
        make_identity(nc, ident_bf[:])

        act_raw = [None] * B_TILES
        emb_raw = [None] * B_TILES

        def load_activations(bt):
            act_raw[bt] = jobs.tile([P, 2, K], BF16, name="cell")
            for operand, source in enumerate((x, h)):
                nc.sync.dma_start(out=act_raw[bt][:, operand, :], in_=source[bt * P : (bt + 1) * P, :])

        def load_embeddings(bt):
            emb_raw[bt] = jobs.tile([P, 3, G * E], BF16, name="state")
            for i, source in enumerate((emb_x, emb_h, emb_b)):
                nc.sync.dma_start(
                    out=emb_raw[bt][:, i, :], in_=source[bt * P : (bt + 1) * P].rearrange("p g e -> p (g e)")
                )

        w_words = [None] * G
        ws_raw = [None] * G
        ws_t = [[None] * 3 for position in range(G)]

        def load_ws(position):
            raws = []
            for i, source in enumerate((Wsx, Wsh, Wsb)):
                raw = per_gate.tile([P, UNIT_BLOCKS, E], BF16, name="ws_raw%d" % i)
                nc.sync.dma_start(out=raw[:], in_=source[GATE_ORDER[position]].rearrange("(j p) e -> p j e", p=P))
                raws.append(raw)
            ws_raw[position] = raws

        def load_words(position, half):
            gate = GATE_ORDER[position]
            if half == 0:
                w_words[position] = per_gate.tile([P, 2, PASSES, H], U32, name="w_words", align_bytes=256)
            first_unit = gate * H + half * N_TILE
            for operand, source in enumerate((Wih_words, Whh_words)):
                for g in range(PASSES):
                    nc.sync.dma_start(
                        out=w_words[position][:, operand, g, half * N_TILE : (half + 1) * N_TILE].bitcast(I32),
                        in_=source[g, :, first_unit : first_unit + N_TILE, :].rearrange("p n t -> p (n t)").bitcast(I32),
                    )

        def load_small_vectors():
            nc.sync.dma_start(out=rows[0 : G * HALVES, :], in_=bias.rearrange("(r n) -> r n", n=N_TILE))
            for i, source in enumerate((ln_gamma, ln_beta)):
                nc.sync.dma_start(
                    out=norm_rows[i * G * UNIT_BLOCKS : (i + 1) * G * UNIT_BLOCKS, :],
                    in_=source.rearrange("g (j p) -> (g j) p", p=P),
                )

        def load_scales(first_column, last_column):
            for operand, source in enumerate((Wih_scales, Whh_scales)):
                for quad in range(4):
                    first = 32 * quad + 8 * operand
                    nc.sync.dma_start(
                        out=planes[first : first + 8, first_column:last_column].bitcast(I32),
                        in_=source[:, 4 * quad : 4 * quad + 4, first_column:last_column].bitcast(I32),
                    )

        def load_gate_scales(position):
            first_column = GATE_ORDER[position] * H
            load_scales(first_column, first_column + H)

        first_column = GATE_ORDER[0] * H
        load_activations(0)
        load_embeddings(0)
        load_ws(0)
        load_scales(first_column, first_column + H)
        load_words(0, 0)
        load_small_vectors()
        load_activations(1)
        load_words(0, 1)
        load_embeddings(1)
        load_activations(2)
        load_embeddings(2)
        load_ws(1)
        load_activations(3)
        load_embeddings(3)
        load_gate_scales(1)
        for half in range(HALVES):
            load_words(1, half)
        bias_spread = [const.tile([P, H], BF16, name="bias_spread%d" % position) for position in range(2)]

        second_gate = GATE_ORDER[1] * H
        nc.sync.dma_start(out=bias_spread[1][:], in_=bias[second_gate : second_gate + H].partition_broadcast(P))
        c_raw = const.tile([P, B_TILES, H], BF16)
        nc.sync.dma_start(out=c_raw[:], in_=c.rearrange("(t p) n -> p t n", p=P))
        gamma_c = const.tile([P, H], BF16)
        nc.sync.dma_start(out=gamma_c[:], in_=lnc_gamma.partition_broadcast(P))
        beta_c = const.tile([P, H], BF16)
        nc.sync.dma_start(out=beta_c[:], in_=lnc_beta.partition_broadcast(P))

        act_codes = const.tile([P, 2, B_TILES, PASSES, P], U32, align_bytes=256)
        act_scales = const.tile([P, 2, B_TILES, PASSES, P], U8, align_bytes=256)
        emb_t = [const.tile([P, 3, G, P], BF16, name="emb_t%d" % bt) for bt in range(B_TILES)]

        def prepare_activations(bt):
            grouped = []
            for operand in range(2):
                words = act_raw[bt][:, operand, :].bitcast(F32)
                flipped = flip_bank([P, PASSES, 2, P], F32)
                for g in range(PASSES):
                    for u in range(2):
                        nc.tensor.transpose(
                            flipped[:, g, u, :], words[:, 256 * g + u : 256 * (g + 1) : 2], ident_f32[:]
                        )
                together = work.tile([P, PASSES * P * 4], BF16, name="grouped%d" % operand, bufs=1, align_bytes=64)
                copy_out = nc.vector.tensor_copy if bt == 0 else nc.scalar.copy
                copy_out(
                    out=together[:].bitcast(F32).rearrange("p (g b u) -> p g b u", g=PASSES, u=2),
                    in_=flipped[:].rearrange("p g u b -> p g b u"),
                )
                grouped.append(together)
            for operand in range(2):
                nc.vector.quantize_mx(
                    out=act_codes[:, operand, bt].rearrange("p g b -> p (g b)").bitcast(FP8X4),
                    scales=act_scales[:, operand, bt].rearrange("p g b -> p (g b)"),
                    in_=grouped[operand][:],
                )

        def prepare_embeddings(bt):
            for i in range(3):
                emb_flip = flip_bank([P, G, P], BF16)
                for gate in range(G):
                    nc.tensor.transpose(emb_flip[:, gate, :], emb_raw[bt][:, i, gate * E : (gate + 1) * E], ident_bf[:])
                nc.scalar.copy(out=emb_t[bt][:, i], in_=emb_flip[:])

        def flip_ws(position, i):
            ws_flip = flip_bank([P, UNIT_BLOCKS, P], BF16)
            for j in range(UNIT_BLOCKS):
                nc.tensor.transpose(ws_flip[:, j, :], ws_raw[position][i][:, j, :], ident_bf[:])
            flat = per_gate.tile([P, H], BF16, name="ws_t%d" % i)
            nc.scalar.copy(out=flat[:], in_=ws_flip[:].rearrange("p j n -> p (j n)"))
            ws_t[position][i] = flat

        c_t = const.tile([P, B_TILES, UNIT_BLOCKS, P], BF16)

        def flip_c(bt):
            c_flip = flip_bank([P, UNIT_BLOCKS, P], BF16)
            for j in range(UNIT_BLOCKS):
                nc.tensor.transpose(c_flip[:, j, :], c_raw[:, bt, j * P : (j + 1) * P], ident_bf[:])
            nc.scalar.copy(out=c_t[:, bt], in_=c_flip[:])

        def bias_by_vector(k):
            job, half = divmod(k, HALVES)
            return job < B_TILES or (job < 2 * B_TILES and half == 0)

        def row_picker(gate, half):
            r = gate * HALVES + half
            return ident_bf[:, r : r + 1].to_broadcast([P, P])

        def spread_first_bias(half):
            repeated = flip_bank([P, N_TILE], F32)
            nc.tensor.matmul(out=repeated[:], lhsT=row_picker(GATE_ORDER[0], half), rhs=rows[:], start=True, stop=True)
            copy_out = nc.scalar.copy if half == 0 else nc.vector.tensor_copy
            copy_out(out=bias_spread[0][:, half * N_TILE : (half + 1) * N_TILE], in_=repeated[:])

        norm_cols = const.tile([P, 2 * G * UNIT_BLOCKS], F32)

        def flip_norm_rows():
            norm_flip = flip_bank([P, P], BF16)
            nc.tensor.transpose(norm_flip[:], norm_rows[:], ident_bf[:])
            nc.vector.tensor_copy(out=norm_cols[:], in_=norm_flip[:, 0 : 2 * G * UNIT_BLOCKS])

        pre = [None] * JOBS
        stats = {}
        banks = {}
        terms = {}

        def gate_of(job):
            return GATE_ORDER[job // B_TILES]

        def columns(half):
            return slice(half * N_TILE, (half + 1) * N_TILE)

        def plain_matmul(k, i, tag):
            job, half = divmod(k, HALVES)
            position, bt = divmod(job, B_TILES)
            gate = GATE_ORDER[position]
            z = psum.tile([P, N_TILE], F32, name=tag)
            with_bias = tag == "zb" and not bias_by_vector(k)
            nc.tensor.matmul(
                out=z[:], lhsT=emb_t[bt][:, i, gate, :], rhs=ws_t[position][i][:, columns(half)],
                start=True, stop=not with_bias,
            )
            if with_bias:
                nc.tensor.matmul(out=z[:], lhsT=row_picker(gate, half), rhs=rows[:], start=False, stop=True)
            banks[tag] = z

        def mx_matmuls(k):
            job, half = divmod(k, HALVES)
            position, bt = divmod(job, B_TILES)
            gate = GATE_ORDER[position]
            for operand, tag in enumerate(("xh", "hh")):
                acc = psum.tile([P, N_TILE], F32, name=tag)
                for g in range(PASSES):
                    first_row = 8 * operand + 4 * g
                    nc.tensor.matmul_mx(
                        out=acc[:],
                        lhsT=act_codes[:, operand, bt, g, :].bitcast(FP8X4),
                        lhsT_scale=act_scales[:, operand, bt, g, :],
                        rhs=w_words[position][:, operand, g, columns(half)].bitcast(FP8X4),
                        rhs_scale=planes[first_row:P, gate * H + half * N_TILE : gate * H + (half + 1) * N_TILE],
                        start=(g == 0),
                        stop=(g == PASSES - 1),
                    )
                banks[tag] = acc
            if half == 0:
                pre[job] = jobs.tile([P, H], F32, name="pre")
                stats[job] = {"parts": small.tile([P, 2 * HALVES], F32, name="parts")}

        def copy_z(k):
            for tag in ("zx", "zh"):
                z_sb = work.tile([P, N_TILE], F32, name=tag + "_sb")
                nc.scalar.copy(out=z_sb[:], in_=banks[tag][:])
                terms[tag] = z_sb

        def leave_psum(tag, other, op):
            term = work.tile([P, N_TILE], F32, name="term_" + tag)
            nc.vector.tensor_tensor(out=term[:], in0=banks[tag][:], in1=other, op=op)
            terms[tag] = term

        def product_h(k):
            job, half = divmod(k, HALVES)
            parts = stats[job]["parts"]
            term = work.tile([P, N_TILE], F32, name="term_hh")
            terms["hh"] = term
            nc.vector.scalar_tensor_tensor(
                out=term[:], in0=banks["hh"][:], scalar=1.0, in1=terms["zh"][:], op0=ALU.mult, op1=ALU.mult,
                accum_out=parts[:, 2 * half : 2 * half + 1],
            )

        def sum_terms(k):
            job, half = divmod(k, HALVES)
            parts = stats[job]["parts"]
            shift = terms["zb"] if bias_by_vector(k) else banks["zb"]
            nc.vector.scalar_tensor_tensor(
                out=terms["xh"][:], in0=shift[:], scalar=1.0, in1=terms["xh"][:], op0=ALU.mult, op1=ALU.add,
                accum_out=parts[:, 2 * half + 1 : 2 * half + 2],
            )
            nc.gpsimd.tensor_tensor(out=pre[job][:, columns(half)], in0=terms["xh"][:], in1=terms["hh"][:], op=ALU.add)

        def norm_mean(key):
            parts = stats[key]["parts"]
            minus_mean = small.tile([P, 1], F32, name="minus_mean")
            scaled = small.tile([P, 2 * HALVES], F32, name="scaled")
            nc.vector.tensor_scalar(
                out=scaled[:, 0 : parts.shape[1]], in0=parts[:], scalar1=-1.0 / H, scalar2=None, op0=ALU.mult, op1=ALU.add,
                accum_out=minus_mean[:],
            )
            stats[key]["minus_mean"] = minus_mean

        def square_job(key, values):
            scatter = small.tile([P, 1], F32, name="scatter")
            scratch = work.tile([P, H], BF16, name="scratch", bufs=2)
            nc.scalar.activation(
                out=scratch[:], in_=values[:], func=ACT.Square, bias=stats[key]["minus_mean"][:, 0:1], accum_out=scatter[:]
            )
            stats[key]["scatter"] = scatter

        def norm_root(key):
            root = small.tile([P, 1], F32, name="root")
            nc.gpsimd.tensor_tensor(out=root[:], in0=stats[key]["scatter"][:], in1=one_half[:], op=ALU.pow)
            padded = small.tile([P, 1], F32, name="padded")
            nc.gpsimd.tensor_scalar(
                out=padded[:], in0=root[:], scalar1=(H - 1) ** -0.5, scalar2=EPS, op0=ALU.mult, op1=ALU.add
            )
            stats[key]["padded"] = padded

        def norm_rstd(key):
            rstd = small.tile([P, 1], F32, name="rstd")
            nc.vector.reciprocal(out=rstd[:], in_=stats[key]["padded"][:])
            stats[key]["rstd"] = rstd

        def centre_times_gamma(key, values, gamma_row):
            nc.vector.scalar_tensor_tensor(
                out=values[:], in0=values[:], scalar=stats[key]["minus_mean"][:, 0:1], in1=gamma_row[:],
                op0=ALU.add, op1=ALU.mult,
            )

        def times_rstd_plus_beta(key, values, beta_row, half):
            nc.vector.scalar_tensor_tensor(
                out=values[:, columns(half)], in0=values[:, columns(half)], scalar=stats[key]["rstd"][:, 0:1],
                in1=beta_row[:, columns(half)], op0=ALU.mult, op1=ALU.add,
            )

        flipped = {}
        acted = [None] * JOBS
        state = [None] * B_TILES
        returned = {}
        cell = [None] * B_TILES
        tanh_c = [None] * B_TILES

        def normalise(job):
            nc.vector.tensor_scalar(
                out=pre[job][:], in0=pre[job][:],
                scalar1=stats[job]["minus_mean"][:, 0:1], scalar2=stats[job]["rstd"][:, 0:1],
                op0=ALU.add, op1=ALU.mult,
            )

        def flip(job, half):
            bank = flip_bank([P, BANK_BLOCKS, P], F32)
            for j in range(BANK_BLOCKS):
                block = half * BANK_BLOCKS + j
                nc.tensor.transpose(bank[:, j, :], pre[job][:, block * P : (block + 1) * P], ident_f32[:])
            flipped[(job, half)] = bank

        def activate(job, half):
            gate = gate_of(job)
            bt = job % B_TILES
            if half == 0 and gate == GATE_I:
                state[bt] = jobs.tile([P, UNIT_BLOCKS, P], F32, name="state")
            if half == 0 and gate != GATE_I:
                acted[job] = jobs.tile([P, UNIT_BLOCKS, P], F32, name="acted", bufs=2)
            target = state[bt] if gate == GATE_I else acted[job]
            for j in range(BANK_BLOCKS):
                block = half * BANK_BLOCKS + j
                column = gate * UNIT_BLOCKS + block
                nc.scalar.activation(
                    out=target[:, block, :],
                    in_=flipped[(job, half)][:, j, :],
                    func=ACT.Tanh if gate == GATE_G else ACT.Sigmoid,
                    scale=norm_cols[:, column : column + 1],
                    bias=norm_cols[:, G * UNIT_BLOCKS + column : G * UNIT_BLOCKS + column + 1],
                )

        def blocks(half):
            return slice(half * BANK_BLOCKS, (half + 1) * BANK_BLOCKS)

        def input_product(job):
            bt = job % B_TILES
            nc.vector.tensor_tensor(out=state[bt][:], in0=state[bt][:], in1=acted[job][:], op=ALU.mult)

        def forget_product(job, half):
            bt = job % B_TILES
            nc.vector.tensor_tensor(
                out=acted[job][:, blocks(half)], in0=acted[job][:, blocks(half)], in1=c_t[:, bt, blocks(half)], op=ALU.mult
            )

        def unflip(name, sources, bt, half):
            bank = flip_bank([P, BANK_BLOCKS, P], F32)
            for j in range(BANK_BLOCKS):
                for i, source in enumerate(sources):
                    nc.tensor.matmul(
                        out=bank[:, j, :], lhsT=source[:, half * BANK_BLOCKS + j, :], rhs=ident_f32[:], is_transpose=True,
                        start=(i == 0), stop=(i == len(sources) - 1),
                    )
            returned[(name, bt, half)] = bank

        def cell_out(bt, half):
            if half == 0:
                cell[bt] = jobs.tile([P, H], F32, name="cell")
                stats[("cell", bt)] = {"parts": small.tile([P, HALVES], F32, name="cell_parts")}
            nc.scalar.activation(
                out=cell[bt][:, columns(half)],
                in_=returned[("cell", bt, half)][:].rearrange("p j n -> p (j n)"),
                func=ACT.Identity,
                accum_out=stats[("cell", bt)]["parts"][:, half : half + 1],
            )

        def cell_tanh(bt, half):
            if half == 0:
                tanh_c[bt] = jobs.tile([P, H], F32, name="state")
            nc.scalar.activation(out=tanh_c[bt][:, columns(half)], in_=cell[bt][:, columns(half)], func=ACT.Tanh)

        def output(job, half):
            bt = job % B_TILES
            pieces = 2 if job == JOBS - 1 and half == HALVES - 1 else 1
            width = N_TILE // pieces
            bank = returned[("o", bt, half)][:].rearrange("p j n -> p (j n)")
            for piece in range(pieces):
                piece_columns = slice(half * N_TILE + piece * width, half * N_TILE + (piece + 1) * width)
                nc.vector.tensor_tensor(
                    out=tanh_c[bt][:, piece_columns], in0=bank[:, piece * width : (piece + 1) * width],
                    in1=tanh_c[bt][:, piece_columns], op=ALU.mult,
                )
                nc.sync.dma_start(out=out_0[bt * P : (bt + 1) * P, piece_columns], in_=tanh_c[bt][:, piece_columns])

        every_gate = GATE_ORDER

        def half_due(k, lag, gates):
            if not 0 <= k - lag < SLOTS:
                return None
            job, half = divmod(k - lag, HALVES)
            return (job, half) if gate_of(job) in gates else None

        def job_due(k, lag, gates):
            due = half_due(k, lag, gates)
            return due[0] if due is not None and due[1] == 0 else None

        def cell_key(job):
            return ("cell", job % B_TILES)

        def small_step(k, gate_lag, cell_lag, step):
            job = None if gate_lag is None else job_due(k, gate_lag, every_gate)
            if job is not None:
                step(job)
            job = None if cell_lag is None else job_due(k, cell_lag, (GATE_F,))
            if job is not None:
                step(cell_key(job))

        idle = psum.tile([P, P], F32, name="xh")

        def keep_clock(count):
            for repeat in range(count):
                nc.tensor.matmul(out=idle[:], lhsT=zeros[:], rhs=zeros[:], start=True, stop=True)

        keep_clock(5)
        prepare_activations(0)
        keep_clock(2)
        prepare_embeddings(0)
        for i in range(3):
            keep_clock(1)
            flip_ws(0, i)

        slots_a_gate = SLOTS // G
        for k in range(SLOTS + LAST_LAG + 1):
            position, step = divmod(k, slots_a_gate)
            issues = k < SLOTS
            half = k % HALVES

            due = half_due(k, LAG_FLIP, every_gate)
            if due is not None:
                flip(due[0], due[1])
            due = half_due(k, LAG_OUTPUT, (GATE_O,))
            if due is not None:
                output(due[0], due[1])
            due = half_due(k, LAG_CELL, (GATE_F,))
            if due is not None:
                forget_product(due[0], due[1])
            job = job_due(k, LAG_CELL + 1, (GATE_G,))
            if job is not None:
                input_product(job)
            job = job_due(k, LAG_NORMALISE, every_gate)
            if job is not None:
                normalise(job)

            if issues:
                plain_matmul(k, 0, "zx")
                plain_matmul(k, 1, "zh")
                copy_z(k)
                mx_matmuls(k)
            if k == 0:
                spread_first_bias(0)
            if k == 2:
                flip_norm_rows()
            job = job_due(k, LAG_SQUARE, every_gate)
            if job is not None:
                square_job(job, pre[job])
            due = half_due(k, LAG_ACTIVATE, every_gate)
            if due is not None:
                activate(due[0], due[1])
            job = job_due(k, LAG_CELL_SQUARE, (GATE_F,))
            if job is not None:
                square_job(cell_key(job), cell[job % B_TILES])
            due = half_due(k, LAG_CELL_TANH, (GATE_F,))
            if due is not None:
                cell_tanh(due[0] % B_TILES, due[1])
            small_step(k, None, LAG_CELL_MEAN, norm_mean)
            if issues:
                leave_psum("xh", terms["zx"][:], ALU.mult)
                product_h(k)
                plain_matmul(k, 2, "zb")

            due = half_due(k, LAG_RETURN, (GATE_O,))
            if due is not None:
                unflip("o", (acted[due[0]],), due[0] % B_TILES, due[1])
            if position == 1 and step < B_TILES:
                flip_c(step)
            ws_steps = FIRST_WS_STEPS if position == 0 else WS_STEPS
            if step in ws_steps and position < G - 1:
                flip_ws(position + 1, ws_steps.index(step))

            due = half_due(k, LAG_CELL_SHIFT, (GATE_F,))
            if due is not None:
                bt = due[0] % B_TILES
                times_rstd_plus_beta(cell_key(due[0]), cell[bt], beta_c, due[1])
                nc.sync.dma_start(out=out_1[bt * P : (bt + 1) * P, columns(due[1])], in_=cell[bt][:, columns(due[1])])
            small_step(k, LAG_MEAN, None, norm_mean)
            small_step(k, LAG_RSTD, LAG_CELL_RSTD, norm_rstd)
            small_step(k, LAG_ROOT, LAG_CELL_ROOT, norm_root)
            if issues:
                if bias_by_vector(k):
                    leave_psum("zb", bias_spread[position][:, columns(half)], ALU.add)
                sum_terms(k)

            if k == 0:
                spread_first_bias(1)

            due = half_due(k, LAG_UNFLIP, (GATE_F,))
            if due is not None:
                unflip("cell", (state[due[0] % B_TILES], acted[due[0]]), due[0] % B_TILES, due[1])
            due = half_due(k, LAG_CELL_OUT, (GATE_F,))
            if due is not None:
                cell_out(due[0] % B_TILES, due[1])
            job = job_due(k, LAG_CELL_NORMALISE, (GATE_F,))
            if job is not None:
                centre_times_gamma(cell_key(job), cell[job % B_TILES], gamma_c)

            if k == SLOTS:
                idle = psum.tile([P, P], F32, name="xh")
            if SLOTS <= k < SLOTS + LAG_RETURN:
                keep_clock(2)

            if k // 2 + 1 < B_TILES:
                if k % 2 == 0:
                    prepare_activations(k // 2 + 1)
                else:
                    prepare_embeddings(k // 2 + 1)
            if step == 1 and 1 <= position < G - 1:
                load_ws(position + 1)
                load_gate_scales(position + 1)
                for half in range(HALVES):
                    load_words(position + 1, half)
